import numpy as np
import ml_dtypes


def mxq(x, axis, fmt="e4m3"):
    dtype, down = {"e4m3": (ml_dtypes.float8_e4m3fn, 7), "e5m2": (ml_dtypes.float8_e5m2, 14)}[fmt]
    v = np.moveaxis(np.asarray(x, np.float32).astype(ml_dtypes.bfloat16).astype(np.float64), axis, -1)
    blocks = v.reshape(v.shape[:-1] + (-1, 32))
    amax = np.abs(blocks).max(-1, keepdims=True)
    byte = np.maximum(np.where(amax > 0, np.frexp(amax)[1] - 1 + 127, 0) - down, 1)
    scale = np.exp2(byte - 127.0)
    codes = (blocks / scale).astype(np.float32).astype(dtype).astype(np.float64)
    return np.moveaxis((codes * scale).reshape(v.shape), -1, axis)


WIDE = False


def mx_kscale(k):
    if not WIDE:
        return np.ones(k)
    levels = np.array([10, -10, 5, -5, 0])
    a = np.random.permutation(np.resize(levels, k // 512 * 4)).reshape(k // 512, 4)
    idx = np.arange(k)
    return np.exp2(a[idx // 512, idx % 128 // 32])


BF16 = ml_dtypes.bfloat16


def bf(x):
    return np.asarray(x, np.float32).astype(BF16)


def f64(x):
    return np.asarray(x).astype(np.float64)


B, T, I, H, U, V = 8, 512, 256, 128, 512, 1024
LECUN_A = 1.7159
LECUN_B = 0.666


def lecun_tanh(v):
    return LECUN_A * np.tanh(LECUN_B * v)


def sigmoid(v):
    return 1.0 / (1.0 + np.exp(-v))


def setup_inputs():
    s = mx_kscale(U)
    return {
        "h1": bf(lecun_tanh(np.random.standard_normal((B, T, U))) * s),
        "ts": bf(np.random.uniform(size=(B, T))),
        "W1": bf(np.random.standard_normal((U, V)) / np.sqrt(U) / s[:, None]),
        "b1": bf(np.random.standard_normal(V) * 0.3),
        "W_ff1": bf(np.random.standard_normal((V, H)) / np.sqrt(V)),
        "b_ff1": bf(np.random.standard_normal(H) * 0.3),
        "W_ff2": bf(np.random.standard_normal((V, H)) / np.sqrt(V)),
        "b_ff2": bf(np.random.standard_normal(H) * 0.3),
        "W_ta": bf(np.random.standard_normal((V, H)) / np.sqrt(V)),
        "b_ta": bf(np.random.standard_normal(H) * 0.3),
        "W_tb": bf(np.random.standard_normal((V, H)) / np.sqrt(V)),
        "b_tb": bf(np.random.standard_normal(H) * 0.3),
    }


def reference(h1, ts, W1, b1, W_ff1, b_ff1, W_ff2, b_ff2, W_ta, b_ta, W_tb, b_tb):
    x = lecun_tanh((mxq(f64(h1), 2, "e4m3") @ mxq(f64(W1), 0, "e4m3")) + f64(b1))
    xq = mxq(x, 2, "e4m3")
    ff1 = np.tanh((xq @ mxq(f64(W_ff1), 0, "e4m3")) + f64(b_ff1))
    ff2 = np.tanh((xq @ mxq(f64(W_ff2), 0, "e4m3")) + f64(b_ff2))
    t_a = (xq @ mxq(f64(W_ta), 0, "e4m3")) + f64(b_ta)
    t_b = (xq @ mxq(f64(W_tb), 0, "e4m3")) + f64(b_tb)
    t_interp = sigmoid(t_a * f64(ts)[:, :, None] + t_b)
    return ff1 * (1.0 - t_interp) + t_interp * ff2

@@ -1,0 +1,390 @@
+from contextlib import ExitStack
+
+import concourse.bass as bass
+import concourse.mybir as mybir
+import concourse.tile as tile
+from concourse.masks import make_identity
+
+F32 = mybir.dt.float32
+BF16 = mybir.dt.bfloat16
+U32 = mybir.dt.uint32
+U8 = mybir.dt.uint8
+FP8X4 = mybir.dt.float8_e4m3fn_x4
+AF = mybir.ActivationFunctionType
+ALU = mybir.AluOpType
+
+P = 128
+NB, T, U, V, H = 8, 512, 512, 1024, 128
+LECUN_A = 1.7159
+LECUN_B = 0.666
+FLOPS = 2 * NB * T * U * V + 2 * NB * T * V * 4 * H
+
+PIN = False
+X_ENG = ("a", "a")
+XO_ENG = "a"
+
+
+def tile_cfccell_pa_t_kernel(
+    tc, h1, ts, W1, b1, W_ff1, b_ff1, W_ff2, b_ff2, W_ta, b_ta, W_tb, b_tb, out
+):
+    nc = tc.nc
+    with ExitStack() as ctx:
+        const = ctx.enter_context(tc.tile_pool(name="const", bufs=1))
+        work = ctx.enter_context(tc.tile_pool(name="work", bufs=3))
+        psum = ctx.enter_context(tc.psum_pool(name="psum", bufs=1))
+        if PIN:
+            ctx.enter_context(tc.manual_schedule())
+
+        h1raw = []
+        for c in range(NB):
+            h1raw.append(const.tile([P, 4, U], BF16, name="h1raw%d" % c))
+        w1raw = const.tile([P, 4, V], BF16, name="w1raw")
+        whraw = const.tile([P, 4, 8, H], BF16, name="whraw")
+        ts_bc = const.tile([P, NB * T], BF16, name="ts_bc")
+        b1raw = const.tile([P, 8], BF16, name="b1raw")
+        bhraw = [const.tile([P, 1], BF16, name="bhraw%d" % k) for k in range(4)]
+
+        def load_h1(c):
+            nc.sync.dma_start(out=h1raw[c][:], in_=h1[c].rearrange("(p r) k -> p r k", r=4))
+
+        def load_w1(g):
+            for u in range(2):
+                nc.sync.dma_start(
+                    out=w1raw[:, 2 * u : 2 * u + 2, 512 * g : 512 * g + 512],
+                    in_=W1[256 * u : 256 * u + 256, 512 * g : 512 * g + 512].rearrange(
+                        "(p e) v -> p e v", e=2
+                    ),
+                )
+
+        heads = (W_ff1, W_ff2, W_ta, W_tb)
+        load_h1(0)
+        load_w1(0)
+        load_w1(1)
+        load_h1(1)
+        for k in range(4):
+            nc.sync.dma_start(
+                out=whraw[:, k, :, :], in_=heads[k].rearrange("(a q) n -> q a n", q=P)
+            )
+        load_h1(2)
+        ts_flat = ts.rearrange("b t -> (b t)")
+        nc.sync.dma_start(
+            out=ts_bc[:, 0 : 4 * T], in_=ts_flat[0 : 4 * T].partition_broadcast(P)
+        )
+        load_h1(3)
+        load_h1(4)
+        nc.sync.dma_start(
+            out=ts_bc[:, 4 * T : 8 * T], in_=ts_flat[4 * T : 8 * T].partition_broadcast(P)
+        )
+        for c in range(5, NB):
+            load_h1(c)
+        with nc.allow_non_contiguous_dma(reason="biases, one element to a partition"):
+            nc.scalar.dma_start(out=b1raw[:], in_=b1.rearrange("(a q) -> q a", q=P))
+            for k, b in enumerate((b_ff1, b_ff2, b_ta, b_tb)):
+                nc.scalar.dma_start(out=bhraw[k][:], in_=b.rearrange("(q o) -> q o", o=1))
+
+        ident = const.tile([P, P], F32, name="ident")
+        make_identity(nc, ident[:])
+        warm = const.tile([P, 1], F32, name="warm")
+        nc.vector.memset(warm[:], 0.0)
+        warm2 = const.tile([P, 1], F32, name="warm2")
+        nc.scalar.activation(out=warm2[:], in_=warm[:], func=AF.Tanh)
+
+        w1grp = const.tile([P, V, 4], BF16, name="w1grp", align_bytes=64)
+        w1c = const.tile([P, V], U32, name="w1c", align_bytes=64)
+        w1s = const.tile([P, V], U8, name="w1s", align_bytes=64)
+        whgrp = const.tile([P, 8, H, 4], BF16, name="whgrp", align_bytes=64)
+        whc = const.tile([P, 8 * H], U32, name="whc", align_bytes=64)
+        whs = const.tile([P, 8 * H], U8, name="whs", align_bytes=64)
+        b1s = const.tile([P, 8], F32, name="b1s")
+        bh = const.tile([P, 4], F32, name="bh")
+
+        def w1_group(g):
+            cols = slice(512 * g, 512 * g + 512)
+            nc.vector.tensor_copy(
+                out=w1grp[:, cols, :].rearrange("p (c i) t -> p c t i", i=4),
+                in_=w1raw[:, :, cols].rearrange("p t (c i) -> p c t i", i=4),
+            )
+
+        def w1_quant(g):
+            cols = slice(512 * g, 512 * g + 512)
+            nc.vector.quantize_mx(
+                out=w1c[:, cols].bitcast(FP8X4),
+                scales=w1s[:, cols],
+                in_=w1grp[:, cols, :].rearrange("p v t -> p (v t)"),
+            )
+
+        def wh_group(half):
+            nc.vector.tensor_copy(
+                out=whgrp[:, 4 * half : 4 * half + 4, :, :],
+                in_=whraw[:, 2 * half : 2 * half + 2, :, :].rearrange(
+                    "p k (g j) n -> p (k g) n j", j=4
+                ),
+            )
+
+        def wh_quant(half):
+            cols = slice(512 * half, 512 * half + 512)
+            nc.vector.quantize_mx(
+                out=whc[:, cols].bitcast(FP8X4),
+                scales=whs[:, cols],
+                in_=whgrp[:, 4 * half : 4 * half + 4, :, :].rearrange("p a n j -> p (a n j)"),
+            )
+
+        def bias_prep():
+            nc.vector.tensor_scalar(
+                out=b1s[:], in0=b1raw[:], scalar1=LECUN_B, scalar2=None, op0=ALU.mult
+            )
+            for k in range(3):
+                nc.vector.tensor_copy(out=bh[:, k : k + 1], in_=bhraw[k][:])
+            nc.vector.tensor_scalar(
+                out=bh[:, 3:4], in0=bhraw[3][:], scalar1=0.5, scalar2=None, op0=ALU.mult
+            )
+
+        st = {}
+
+        def copy_out(eng, dst, src):
+            if eng == "a":
+                nc.scalar.copy(out=dst, in_=src)
+            else:
+                nc.vector.tensor_copy(out=dst, in_=src)
+
+        def T_in(c):
+            words = h1raw[c][:].bitcast(F32)
+            for half in range(2):
+                tr = psum.tile([P, 2, 256], F32, name="tr", tag="tr", bufs=2)
+                for rr in range(2):
+                    for u in range(2):
+                        nc.tensor.transpose(
+                            tr[:, u, P * rr : P * rr + P],
+                            words[:, 2 * half + rr, P * u : P * u + P],
+                            ident[:],
+                        )
+                st[("tr", c, half)] = tr
+
+        def X_in(c):
+            h1grp = work.tile([P, T, 4], BF16, name="h1grp", tag="h1grp", bufs=2, align_bytes=64)
+            st[("h1grp", c)] = h1grp
+            g32 = h1grp[:].bitcast(F32)
+            for half in range(2):
+                copy_out(
+                    X_ENG[half],
+                    g32[:, 256 * half : 256 * half + 256, :],
+                    st[("tr", c, half)][:].rearrange("p u w -> p w u"),
+                )
+
+        def Q1(c):
+            h1c = work.tile([P, T], U32, name="h1c", tag="h1c", bufs=2, align_bytes=64)
+            h1s = work.tile([P, T], U8, name="h1s", tag="h1s", bufs=2, align_bytes=64)
+            nc.vector.quantize_mx(
+                out=h1c[:].bitcast(FP8X4),
+                scales=h1s[:],
+                in_=st[("h1grp", c)][:].rearrange("p w t -> p (w t)"),
+            )
+            st[("h1c", c)] = (h1c, h1s)
+
+        def P1(c, g, j):
+            h1c, h1s = st[("h1c", c)]
+            acc = psum.tile([P, T], F32, name="s1", tag="s1", bufs=3)
+            cols = slice(P * (4 * g + j), P * (4 * g + j) + P)
+            nc.tensor.matmul_mx(
+                out=acc[:],
+                lhsT=w1c[:, cols].bitcast(FP8X4),
+                lhsT_scale=w1s[:, cols],
+                rhs=h1c[:].bitcast(FP8X4),
+                rhs_scale=h1s[:],
+                start=True,
+                stop=True,
+            )
+            st[("s1", c, g, j)] = acc
+
+        def A1(c, g, j):
+            if j == 0:
+                st[("th1", c, g)] = work.tile([P, 4, T], F32, name="th1", tag="th1", bufs=3)
+            nc.scalar.activation(
+                out=st[("th1", c, g)][:, j, :],
+                in_=st[("s1", c, g, j)][:],
+                func=AF.Tanh,
+                bias=b1s[:, 4 * g + j : 4 * g + j + 1],
+                scale=LECUN_B,
+            )
+
+        def M(c, g):
+            xgrp = work.tile([P, T, 4], BF16, name="xgrp", tag="xgrp", bufs=3, align_bytes=64)
+            nc.vector.tensor_scalar(
+                out=xgrp[:],
+                in0=st[("th1", c, g)][:].rearrange("p j w -> p w j"),
+                scalar1=LECUN_A,
+                scalar2=None,
+                op0=ALU.mult,
+            )
+            st[("xgrp", c, g)] = xgrp
+
+        def Q2(c, g):
+            xc = work.tile([P, T], U32, name="xc", tag="xc%d" % g, bufs=3, align_bytes=64)
+            xs = work.tile([P, T], U8, name="xs", tag="xs%d" % g, bufs=3, align_bytes=64)
+            nc.vector.quantize_mx(
+                out=xc[:].bitcast(FP8X4),
+                scales=xs[:],
+                in_=st[("xgrp", c, g)][:].rearrange("p w t -> p (w t)"),
+            )
+            st[("xc", c, g)] = (xc, xs)
+
+        def S2(c, k):
+            acc = psum.tile([P, T], F32, name="s2", tag="s2", bufs=3)
+            for g in range(2):
+                xc, xs = st[("xc", c, g)]
+                cols = slice(P * (2 * k + g), P * (2 * k + g) + P)
+                nc.tensor.matmul_mx(
+                    out=acc[:],
+                    lhsT=whc[:, cols].bitcast(FP8X4),
+                    lhsT_scale=whs[:, cols],
+                    rhs=xc[:].bitcast(FP8X4),
+                    rhs_scale=xs[:],
+                    start=(g == 0),
+                    stop=(g == 1),
+                )
+            st[("s2", c, k)] = acc
+
+        def FF(c, k):
+            ff = work.tile([P, T], F32, name="ff", tag="ff%d" % k, bufs=3)
+            nc.scalar.activation(
+                out=ff[:], in_=st[("s2", c, k)][:], func=AF.Tanh, bias=bh[:, k : k + 1], scale=1.0
+            )
+            st[("ff", c, k)] = ff
+
+        def Ea(c):
+            u = work.tile([P, T], F32, name="u", tag="u", bufs=2)
+            nc.vector.scalar_tensor_tensor(
+                out=u[:].rearrange("q (r p) -> q r p", r=4),
+                in0=st[("s2", c, 2)][:].rearrange("q (r p) -> q r p", r=4),
+                scalar=bh[:, 2:3],
+                in1=ts_bc[:, T * c : T * c + T].rearrange("q (p r) -> q r p", r=4),
+                op0=ALU.add,
+                op1=ALU.mult,
+            )
+            st[("u", c)] = u
+
+        def Eb(c):
+            v = work.tile([P, T], F32, name="v", tag="v", bufs=2)
+            nc.vector.tensor_tensor(out=v[:], in0=st[("u", c)][:], in1=st[("s2", c, 3)][:], op=ALU.add)
+            st[("v", c)] = v
+
+        def TH(c):
+            th = work.tile([P, T], F32, name="th", tag="th", bufs=2)
+            nc.scalar.activation(
+                out=th[:], in_=st[("v", c)][:], func=AF.Tanh, bias=bh[:, 3:4], scale=0.5
+            )
+            st[("th", c)] = th
+
+        def Ec(c):
+            d = work.tile([P, T], F32, name="d", tag="d", bufs=2)
+            nc.vector.tensor_tensor(
+                out=d[:], in0=st[("ff", c, 1)][:], in1=st[("ff", c, 0)][:], op=ALU.subtract
+            )
+            st[("d", c)] = d
+
+        def Em(c):
+            m = work.tile([P, T], F32, name="m", tag="m", bufs=2)
+            nc.vector.scalar_tensor_tensor(
+                out=m[:], in0=st[("th", c)][:], scalar=1.0, in1=st[("d", c)][:],
+                op0=ALU.add, op1=ALU.mult,
+            )
+            st[("m", c)] = m
+
+        def Eo(c):
+            o = work.tile([P, T], F32, name="o", tag="o", bufs=2)
+            nc.vector.scalar_tensor_tensor(
+                out=o[:], in0=st[("m", c)][:], scalar=0.5, in1=st[("ff", c, 0)][:],
+                op0=ALU.mult, op1=ALU.add,
+            )
+            st[("o", c)] = o
+
+        def TO(c):
+            tro = psum.tile([P, 4, H], F32, name="tro", tag="tr", bufs=2)
+            for r in range(4):
+                nc.tensor.transpose(tro[:, r, :], st[("o", c)][:, P * r : P * r + P], ident[:])
+            st[("tro", c)] = tro
+
+        def XO(c):
+            osb = work.tile([P, 4, H], F32, name="osb", tag="osb", bufs=3)
+            copy_out(XO_ENG, osb[:], st[("tro", c)][:])
+            nc.sync.dma_start(out=out[c].rearrange("(p r) h -> p r h", r=4), in_=osb[:])
+
+        def ok(c):
+            return 0 <= c < NB
+
+        T_in(0)
+        X_in(0)
+        bias_prep()
+        w1_group(0)
+        Q1(0)
+        w1_quant(0)
+        w1_group(1)
+        for j in range(3):
+            P1(0, 0, j)
+        w1_quant(1)
+
+        for i in range(NB + 2):
+            if ok(i + 1):
+                T_in(i + 1)
+            if ok(i):
+                A1(i, 0, 0)
+                P1(i, 0, 3)
+            if ok(i - 2):
+                Ec(i - 2)
+            if ok(i):
+                A1(i, 0, 1)
+                P1(i, 1, 0)
+            if ok(i - 1):
+                Q2(i - 1, 1)
+            if ok(i):
+                A1(i, 0, 2)
+                P1(i, 1, 1)
+            if ok(i - 2):
+                Em(i - 2)
+                Eo(i - 2)
+            if ok(i):
+                A1(i, 0, 3)
+            if ok(i - 1):
+                S2(i - 1, 0)
+            if ok(i):
+                P1(i, 1, 2)
+            if ok(i - 1):
+                S2(i - 1, 1)
+            if ok(i + 1):
+                X_in(i + 1)
+            if ok(i):
+                M(i, 0)
+            if ok(i - 2):
+                TO(i - 2)
+            if ok(i - 1):
+                FF(i - 1, 0)
+                FF(i - 1, 1)
+                S2(i - 1, 2)
+                S2(i - 1, 3)
+            if ok(i + 1):
+                Q1(i + 1)
+            if ok(i - 1):
+                Ea(i - 1)
+            if ok(i):
+                Q2(i, 0)
+            if i == 0:
+                wh_group(0)
+                wh_group(1)
+            if ok(i - 1):
+                Eb(i - 1)
+            if ok(i):
+                A1(i, 1, 0)
+                P1(i, 1, 3)
+                for j in range(3):
+                    A1(i, 1, j + 1)
+                    if ok(i + 1):
+                        P1(i + 1, 0, j)
+            if ok(i - 2):
+                XO(i - 2)
+            if ok(i - 1):
+                TH(i - 1)
+            if ok(i):
+                M(i, 1)
+            if i == 0:
+                wh_quant(0)
+                wh_quant(1)

@@ -19,7 +19,7 @@ LECUN_A = 1.7159
 LECUN_B = 0.666
 FLOPS = 2 * NB * T * U * V + 2 * NB * T * V * 4 * H
 
-PIN = False
+PIN = True
 X_ENG = ("a", "a")
 XO_ENG = "a"
 
@@ -57,10 +57,14 @@ def tile_cfccell_pa_t_kernel(
                 )
 
         heads = (W_ff1, W_ff2, W_ta, W_tb)
-        load_h1(0)
+        h1_0 = h1[0].rearrange("(p r) k -> p r k", r=4)
+        for half in range(2):
+            nc.sync.dma_start(
+                out=h1raw[0][:, 2 * half : 2 * half + 2, :], in_=h1_0[:, 2 * half : 2 * half + 2, :]
+            )
         load_w1(0)
-        load_w1(1)
         load_h1(1)
+        load_w1(1)
         for k in range(4):
             nc.sync.dma_start(
                 out=whraw[:, k, :, :], in_=heads[k].rearrange("(a q) n -> q a n", q=P)
@@ -98,15 +102,15 @@ def tile_cfccell_pa_t_kernel(
         b1s = const.tile([P, 8], F32, name="b1s")
         bh = const.tile([P, 4], F32, name="bh")
 
-        def w1_group(g):
-            cols = slice(512 * g, 512 * g + 512)
+        def w1_group(k):
+            cols = slice(P * k, P * k + P)
             nc.vector.tensor_copy(
                 out=w1grp[:, cols, :].rearrange("p (c i) t -> p c t i", i=4),
                 in_=w1raw[:, :, cols].rearrange("p t (c i) -> p c t i", i=4),
             )
 
-        def w1_quant(g):
-            cols = slice(512 * g, 512 * g + 512)
+        def w1_quant(k):
+            cols = slice(P * k, P * k + P)
             nc.vector.quantize_mx(
                 out=w1c[:, cols].bitcast(FP8X4),
                 scales=w1s[:, cols],
@@ -133,7 +137,10 @@ def tile_cfccell_pa_t_kernel(
             nc.vector.tensor_scalar(
                 out=b1s[:], in0=b1raw[:], scalar1=LECUN_B, scalar2=None, op0=ALU.mult
             )
-            for k in range(3):
+            nc.vector.tensor_scalar(
+                out=bh[:, 0:1], in0=bhraw[0][:], scalar1=-1.0, scalar2=None, op0=ALU.mult
+            )
+            for k in range(1, 3):
                 nc.vector.tensor_copy(out=bh[:, k : k + 1], in_=bhraw[k][:])
             nc.vector.tensor_scalar(
                 out=bh[:, 3:4], in0=bhraw[3][:], scalar1=0.5, scalar2=None, op0=ALU.mult
@@ -150,7 +157,7 @@ def tile_cfccell_pa_t_kernel(
         def T_in(c):
             words = h1raw[c][:].bitcast(F32)
             for half in range(2):
-                tr = psum.tile([P, 2, 256], F32, name="tr", tag="tr", bufs=2)
+                tr = psum.tile([P, 2, 256], F32, name="tr", tag="tr", bufs=3)
                 for rr in range(2):
                     for u in range(2):
                         nc.tensor.transpose(
@@ -166,7 +173,7 @@ def tile_cfccell_pa_t_kernel(
             g32 = h1grp[:].bitcast(F32)
             for half in range(2):
                 copy_out(
-                    X_ENG[half],
+                    "v" if (c == 0 and half == 1) else X_ENG[half],
                     g32[:, 256 * half : 256 * half + 256, :],
                     st[("tr", c, half)][:].rearrange("p u w -> p w u"),
                 )
@@ -183,7 +190,7 @@ def tile_cfccell_pa_t_kernel(
 
         def P1(c, g, j):
             h1c, h1s = st[("h1c", c)]
-            acc = psum.tile([P, T], F32, name="s1", tag="s1", bufs=3)
+            acc = psum.tile([P, T], F32, name="s1", tag="mm", bufs=5)
             cols = slice(P * (4 * g + j), P * (4 * g + j) + P)
             nc.tensor.matmul_mx(
                 out=acc[:],
@@ -210,8 +217,8 @@ def tile_cfccell_pa_t_kernel(
         def M(c, g):
             xgrp = work.tile([P, T, 4], BF16, name="xgrp", tag="xgrp", bufs=3, align_bytes=64)
             nc.vector.tensor_scalar(
-                out=xgrp[:],
-                in0=st[("th1", c, g)][:].rearrange("p j w -> p w j"),
+                out=xgrp[:].rearrange("p (c i) j -> p c j i", i=4),
+                in0=st[("th1", c, g)][:].rearrange("p j (c i) -> p c j i", i=4),
                 scalar1=LECUN_A,
                 scalar2=None,
                 op0=ALU.mult,
@@ -219,8 +226,8 @@ def tile_cfccell_pa_t_kernel(
             st[("xgrp", c, g)] = xgrp
 
         def Q2(c, g):
-            xc = work.tile([P, T], U32, name="xc", tag="xc%d" % g, bufs=3, align_bytes=64)
-            xs = work.tile([P, T], U8, name="xs", tag="xs%d" % g, bufs=3, align_bytes=64)
+            xc = work.tile([P, T], U32, name="xc", tag="xc%d" % g, bufs=4, align_bytes=64)
+            xs = work.tile([P, T], U8, name="xs", tag="xs%d" % g, bufs=4, align_bytes=64)
             nc.vector.quantize_mx(
                 out=xc[:].bitcast(FP8X4),
                 scales=xs[:],
@@ -229,7 +236,7 @@ def tile_cfccell_pa_t_kernel(
             st[("xc", c, g)] = (xc, xs)
 
         def S2(c, k):
-            acc = psum.tile([P, T], F32, name="s2", tag="s2", bufs=3)
+            acc = psum.tile([P, T], F32, name="s2", tag="mm", bufs=5)
             for g in range(2):
                 xc, xs = st[("xc", c, g)]
                 cols = slice(P * (2 * k + g), P * (2 * k + g) + P)
@@ -247,7 +254,8 @@ def tile_cfccell_pa_t_kernel(
         def FF(c, k):
             ff = work.tile([P, T], F32, name="ff", tag="ff%d" % k, bufs=3)
             nc.scalar.activation(
-                out=ff[:], in_=st[("s2", c, k)][:], func=AF.Tanh, bias=bh[:, k : k + 1], scale=1.0
+                out=ff[:], in_=st[("s2", c, k)][:], func=AF.Tanh, bias=bh[:, k : k + 1],
+                scale=(-1.0 if k == 0 else 1.0),
             )
             st[("ff", c, k)] = ff
 
@@ -264,127 +272,124 @@ def tile_cfccell_pa_t_kernel(
             st[("u", c)] = u
 
         def Eb(c):
-            v = work.tile([P, T], F32, name="v", tag="v", bufs=2)
+            v = work.tile([P, T], F32, name="v", tag="v", bufs=3)
             nc.vector.tensor_tensor(out=v[:], in0=st[("u", c)][:], in1=st[("s2", c, 3)][:], op=ALU.add)
             st[("v", c)] = v
 
         def TH(c):
-            th = work.tile([P, T], F32, name="th", tag="th", bufs=2)
+            th = work.tile([P, T], F32, name="th", tag="th", bufs=3)
             nc.scalar.activation(
                 out=th[:], in_=st[("v", c)][:], func=AF.Tanh, bias=bh[:, 3:4], scale=0.5
             )
             st[("th", c)] = th
 
-        def Ec(c):
-            d = work.tile([P, T], F32, name="d", tag="d", bufs=2)
-            nc.vector.tensor_tensor(
-                out=d[:], in0=st[("ff", c, 1)][:], in1=st[("ff", c, 0)][:], op=ALU.subtract
-            )
-            st[("d", c)] = d
-
         def Em(c):
-            m = work.tile([P, T], F32, name="m", tag="m", bufs=2)
+            e1 = work.tile([P, T], F32, name="e1", tag="e1", bufs=2)
             nc.vector.scalar_tensor_tensor(
-                out=m[:], in0=st[("th", c)][:], scalar=1.0, in1=st[("d", c)][:],
-                op0=ALU.add, op1=ALU.mult,
+                out=e1[:], in0=st[("th", c)][:], scalar=1.0, in1=st[("ff", c, 0)][:],
+                op0=ALU.subtract, op1=ALU.mult,
             )
-            st[("m", c)] = m
+            st[("e1", c)] = e1
 
         def Eo(c):
-            o = work.tile([P, T], F32, name="o", tag="o", bufs=2)
+            e2 = work.tile([P, T], F32, name="e2", tag="e2", bufs=2)
             nc.vector.scalar_tensor_tensor(
-                out=o[:], in0=st[("m", c)][:], scalar=0.5, in1=st[("ff", c, 0)][:],
-                op0=ALU.mult, op1=ALU.add,
+                out=e2[:], in0=st[("th", c)][:], scalar=1.0, in1=st[("ff", c, 1)][:],
+                op0=ALU.add, op1=ALU.mult,
             )
-            st[("o", c)] = o
+            st[("e2", c)] = e2
 
         def TO(c):
-            tro = psum.tile([P, 4, H], F32, name="tro", tag="tr", bufs=2)
+            tro = psum.tile([P, 4, H], F32, name="tro", tag="tr", bufs=3)
             for r in range(4):
-                nc.tensor.transpose(tro[:, r, :], st[("o", c)][:, P * r : P * r + P], ident[:])
+                nc.tensor.matmul(
+                    out=tro[:, r, :], lhsT=st[("e1", c)][:, P * r : P * r + P], rhs=ident[:],
+                    start=True, stop=False, is_transpose=True,
+                )
+                nc.tensor.matmul(
+                    out=tro[:, r, :], lhsT=st[("e2", c)][:, P * r : P * r + P], rhs=ident[:],
+                    start=False, stop=True, is_transpose=True,
+                )
             st[("tro", c)] = tro
 
         def XO(c):
             osb = work.tile([P, 4, H], F32, name="osb", tag="osb", bufs=3)
-            copy_out(XO_ENG, osb[:], st[("tro", c)][:])
+            nc.scalar.mul(out=osb[:], in_=st[("tro", c)][:], mul=0.5)
             nc.sync.dma_start(out=out[c].rearrange("(p r) h -> p r h", r=4), in_=osb[:])
 
         def ok(c):
             return 0 <= c < NB
+
+        LS, LT, LE, LO = 2, 3, 4, 5
 
         T_in(0)
         X_in(0)
         bias_prep()
         w1_group(0)
         Q1(0)
-        w1_quant(0)
         w1_group(1)
-        for j in range(3):
-            P1(0, 0, j)
-        w1_quant(1)
+        w1_quant(0)
+        for k in range(2, 8):
+            w1_group(k)
+            w1_quant(k - 1)
+            if k < 5:
+                P1(0, 0, k - 2)
+        w1_quant(7)
 
-        for i in range(NB + 2):
+        for i in range(NB + LO):
+            c = i - LS
+            if ok(i):
+                P1(i, 0, 3)
+            if ok(i - LO):
+                TO(i - LO)
             if ok(i + 1):
                 T_in(i + 1)
             if ok(i):
                 A1(i, 0, 0)
-                P1(i, 0, 3)
-            if ok(i - 2):
-                Ec(i - 2)
-            if ok(i):
-                A1(i, 0, 1)
-                P1(i, 1, 0)
+            if ok(i - LE):
+                Em(i - LE)
+                Eo(i - LE)
             if ok(i - 1):
                 Q2(i - 1, 1)
+            if ok(c):
+                S2(c, 2)
+                S2(c, 3)
             if ok(i):
-                A1(i, 0, 2)
-                P1(i, 1, 1)
-            if ok(i - 2):
-                Em(i - 2)
-                Eo(i - 2)
-            if ok(i):
-                A1(i, 0, 3)
-            if ok(i - 1):
-                S2(i - 1, 0)
-            if ok(i):
-                P1(i, 1, 2)
-            if ok(i - 1):
-                S2(i - 1, 1)
+                for j in range(3):
+                    A1(i, 0, j + 1)
+                    P1(i, 1, j)
+            if ok(c):
+                Ea(c)
+                Eb(c)
+            if ok(i - LO):
+                XO(i - LO)
+            if ok(i - LT):
+                TH(i - LT)
             if ok(i + 1):
                 X_in(i + 1)
             if ok(i):
                 M(i, 0)
-            if ok(i - 2):
-                TO(i - 2)
-            if ok(i - 1):
-                FF(i - 1, 0)
-                FF(i - 1, 1)
-                S2(i - 1, 2)
-                S2(i - 1, 3)
             if ok(i + 1):
                 Q1(i + 1)
-            if ok(i - 1):
-                Ea(i - 1)
             if ok(i):
                 Q2(i, 0)
-            if i == 0:
-                wh_group(0)
-                wh_group(1)
-            if ok(i - 1):
-                Eb(i - 1)
+            if i < 2:
+                wh_group(i)
             if ok(i):
                 A1(i, 1, 0)
                 P1(i, 1, 3)
+            if ok(c):
+                S2(c, 0)
+                S2(c, 1)
+            if ok(i):
                 for j in range(3):
                     A1(i, 1, j + 1)
                     if ok(i + 1):
                         P1(i + 1, 0, j)
-            if ok(i - 2):
-                XO(i - 2)
-            if ok(i - 1):
-                TH(i - 1)
+            if ok(c):
+                FF(c, 0)
+                FF(c, 1)
             if ok(i):
                 M(i, 1)
-            if i == 0:
-                wh_quant(0)
-                wh_quant(1)
+            if i < 2:
+                wh_quant(i)

@@ -57,6 +57,8 @@ def tile_cfccell_pa_t_kernel(
                 )
 
         heads = (W_ff1, W_ff2, W_ta, W_tb)
+        with nc.allow_non_contiguous_dma(reason="b1, one element of each 128 to a partition"):
+            nc.scalar.dma_start(out=b1raw[:], in_=b1.rearrange("(a q) -> q a", q=P))
         h1_0 = h1[0].rearrange("(p r) k -> p r k", r=4)
         for half in range(2):
             nc.sync.dma_start(
@@ -81,13 +83,12 @@ def tile_cfccell_pa_t_kernel(
         )
         for c in range(5, NB):
             load_h1(c)
-        with nc.allow_non_contiguous_dma(reason="biases, one element to a partition"):
-            nc.scalar.dma_start(out=b1raw[:], in_=b1.rearrange("(a q) -> q a", q=P))
-            for k, b in enumerate((b_ff1, b_ff2, b_ta, b_tb)):
-                nc.scalar.dma_start(out=bhraw[k][:], in_=b.rearrange("(q o) -> q o", o=1))
 
         ident = const.tile([P, P], F32, name="ident")
         make_identity(nc, ident[:])
+        with nc.allow_non_contiguous_dma(reason="head biases, one element to a partition"):
+            for k, b in enumerate((b_ff1, b_ff2, b_ta, b_tb)):
+                nc.gpsimd.dma_start(out=bhraw[k][:], in_=b.rearrange("(q o) -> q o", o=1))
         warm = const.tile([P, 1], F32, name="warm")
         nc.vector.memset(warm[:], 0.0)
         warm2 = const.tile([P, 1], F32, name="warm2")
@@ -133,10 +134,12 @@ def tile_cfccell_pa_t_kernel(
                 in_=whgrp[:, 4 * half : 4 * half + 4, :, :].rearrange("p a n j -> p (a n j)"),
             )
 
-        def bias_prep():
+        def b1_prep():
             nc.vector.tensor_scalar(
                 out=b1s[:], in0=b1raw[:], scalar1=LECUN_B, scalar2=None, op0=ALU.mult
             )
+
+        def bias_prep():
             nc.vector.tensor_scalar(
                 out=bh[:, 0:1], in0=bhraw[0][:], scalar1=-1.0, scalar2=None, op0=ALU.mult
             )
@@ -324,7 +327,7 @@ def tile_cfccell_pa_t_kernel(
 
         T_in(0)
         X_in(0)
-        bias_prep()
+        b1_prep()
         w1_group(0)
         Q1(0)
         w1_group(1)
@@ -375,6 +378,8 @@ def tile_cfccell_pa_t_kernel(
                 Q2(i, 0)
             if i < 2:
                 wh_group(i)
+            if i == 0:
+                bias_prep()
             if ok(i):
                 A1(i, 1, 0)
                 P1(i, 1, 3)

@@ -15,13 +15,10 @@ ALU = mybir.AluOpType
 
 P = 128
 NB, T, U, V, H = 8, 512, 512, 1024, 128
+R = T // P
 LECUN_A = 1.7159
 LECUN_B = 0.666
 FLOPS = 2 * NB * T * U * V + 2 * NB * T * V * 4 * H
-
-PIN = True
-X_ENG = ("a", "a")
-XO_ENG = "a"
 
 
 def tile_cfccell_pa_t_kernel(
@@ -32,57 +29,61 @@ def tile_cfccell_pa_t_kernel(
         const = ctx.enter_context(tc.tile_pool(name="const", bufs=1))
         work = ctx.enter_context(tc.tile_pool(name="work", bufs=3))
         psum = ctx.enter_context(tc.psum_pool(name="psum", bufs=1))
-        if PIN:
-            ctx.enter_context(tc.manual_schedule())
+        ctx.enter_context(tc.manual_schedule())
 
-        h1raw = []
-        for c in range(NB):
-            h1raw.append(const.tile([P, 4, U], BF16, name="h1raw%d" % c))
-        w1raw = const.tile([P, 4, V], BF16, name="w1raw")
-        whraw = const.tile([P, 4, 8, H], BF16, name="whraw")
-        ts_bc = const.tile([P, NB * T], BF16, name="ts_bc")
+        h1raw = [const.tile([P, R, U], BF16, name="h1raw%d" % c) for c in range(NB)]
+        w1raw = [const.tile([P, 4, V // 2], BF16, name="w1raw%d" % g) for g in range(2)]
+        whraw = [const.tile([P, 2, 8, H], BF16, name="whraw%d" % p) for p in range(2)]
+        ts_bc = [const.tile([P, 4 * T], BF16, name="ts_bc%d" % q) for q in range(2)]
         b1raw = const.tile([P, 8], BF16, name="b1raw")
         bhraw = [const.tile([P, 1], BF16, name="bhraw%d" % k) for k in range(4)]
+        ts_flat = ts.rearrange("b t -> (b t)")
+        heads = (W_ff1, W_ff2, W_ta, W_tb)
 
-        def load_h1(c):
-            nc.sync.dma_start(out=h1raw[c][:], in_=h1[c].rearrange("(p r) k -> p r k", r=4))
+        def load_h1(c, r0, r1):
+            nc.sync.dma_start(
+                out=h1raw[c][:, r0:r1, :],
+                in_=h1[c].rearrange("(p r) k -> p r k", r=R)[:, r0:r1, :],
+            )
 
         def load_w1(g):
             for u in range(2):
                 nc.sync.dma_start(
-                    out=w1raw[:, 2 * u : 2 * u + 2, 512 * g : 512 * g + 512],
+                    out=w1raw[g][:, 2 * u : 2 * u + 2, :],
                     in_=W1[256 * u : 256 * u + 256, 512 * g : 512 * g + 512].rearrange(
                         "(p e) v -> p e v", e=2
                     ),
                 )
 
-        heads = (W_ff1, W_ff2, W_ta, W_tb)
+        def load_wh(pair):
+            for k in range(2):
+                nc.sync.dma_start(
+                    out=whraw[pair][:, k, :, :],
+                    in_=heads[2 * pair + k].rearrange("(a q) n -> q a n", q=P),
+                )
+
+        def load_ts(q):
+            nc.sync.dma_start(
+                out=ts_bc[q][:],
+                in_=ts_flat[4 * T * q : 4 * T * q + 4 * T].partition_broadcast(P),
+            )
+
         with nc.allow_non_contiguous_dma(reason="b1, one element of each 128 to a partition"):
             nc.scalar.dma_start(out=b1raw[:], in_=b1.rearrange("(a q) -> q a", q=P))
-        h1_0 = h1[0].rearrange("(p r) k -> p r k", r=4)
-        for half in range(2):
-            nc.sync.dma_start(
-                out=h1raw[0][:, 2 * half : 2 * half + 2, :], in_=h1_0[:, 2 * half : 2 * half + 2, :]
-            )
+        load_h1(0, 0, 2)
+        load_h1(0, 2, 4)
         load_w1(0)
-        load_h1(1)
         load_w1(1)
-        for k in range(4):
-            nc.sync.dma_start(
-                out=whraw[:, k, :, :], in_=heads[k].rearrange("(a q) n -> q a n", q=P)
-            )
-        load_h1(2)
-        ts_flat = ts.rearrange("b t -> (b t)")
-        nc.sync.dma_start(
-            out=ts_bc[:, 0 : 4 * T], in_=ts_flat[0 : 4 * T].partition_broadcast(P)
-        )
-        load_h1(3)
-        load_h1(4)
-        nc.sync.dma_start(
-            out=ts_bc[:, 4 * T : 8 * T], in_=ts_flat[4 * T : 8 * T].partition_broadcast(P)
-        )
+        load_h1(1, 0, 4)
+        load_wh(1)
+        load_h1(2, 0, 4)
+        load_wh(0)
+        load_ts(0)
+        load_h1(3, 0, 4)
+        load_h1(4, 0, 4)
+        load_ts(1)
         for c in range(5, NB):
-            load_h1(c)
+            load_h1(c, 0, 4)
 
         ident = const.tile([P, P], F32, name="ident")
         make_identity(nc, ident[:])
@@ -107,7 +108,9 @@ def tile_cfccell_pa_t_kernel(
             cols = slice(P * k, P * k + P)
             nc.vector.tensor_copy(
                 out=w1grp[:, cols, :].rearrange("p (c i) t -> p c t i", i=4),
-                in_=w1raw[:, :, cols].rearrange("p t (c i) -> p c t i", i=4),
+                in_=w1raw[k // 4][:, :, P * (k % 4) : P * (k % 4) + P].rearrange(
+                    "p t (c i) -> p c t i", i=4
+                ),
             )
 
         def w1_quant(k):
@@ -118,20 +121,18 @@ def tile_cfccell_pa_t_kernel(
                 in_=w1grp[:, cols, :].rearrange("p v t -> p (v t)"),
             )
 
-        def wh_group(half):
+        def wh_group(pair):
             nc.vector.tensor_copy(
-                out=whgrp[:, 4 * half : 4 * half + 4, :, :],
-                in_=whraw[:, 2 * half : 2 * half + 2, :, :].rearrange(
-                    "p k (g j) n -> p (k g) n j", j=4
-                ),
+                out=whgrp[:, 4 * pair : 4 * pair + 4, :, :],
+                in_=whraw[pair][:].rearrange("p k (g j) n -> p (k g) n j", j=4),
             )
 
-        def wh_quant(half):
-            cols = slice(512 * half, 512 * half + 512)
+        def wh_quant(pair):
+            cols = slice(512 * pair, 512 * pair + 512)
             nc.vector.quantize_mx(
                 out=whc[:, cols].bitcast(FP8X4),
                 scales=whs[:, cols],
-                in_=whgrp[:, 4 * half : 4 * half + 4, :, :].rearrange("p a n j -> p (a n j)"),
+                in_=whgrp[:, 4 * pair : 4 * pair + 4, :, :].rearrange("p a n j -> p (a n j)"),
             )
 
         def b1_prep():
@@ -143,19 +144,10 @@ def tile_cfccell_pa_t_kernel(
             nc.vector.tensor_scalar(
                 out=bh[:, 0:1], in0=bhraw[0][:], scalar1=-1.0, scalar2=None, op0=ALU.mult
             )
-            for k in range(1, 3):
+            for k in range(1, 4):
                 nc.vector.tensor_copy(out=bh[:, k : k + 1], in_=bhraw[k][:])
-            nc.vector.tensor_scalar(
-                out=bh[:, 3:4], in0=bhraw[3][:], scalar1=0.5, scalar2=None, op0=ALU.mult
-            )
 
         st = {}
-
-        def copy_out(eng, dst, src):
-            if eng == "a":
-                nc.scalar.copy(out=dst, in_=src)
-            else:
-                nc.vector.tensor_copy(out=dst, in_=src)
 
         def T_in(c):
             words = h1raw[c][:].bitcast(F32)
@@ -170,16 +162,17 @@ def tile_cfccell_pa_t_kernel(
                         )
                 st[("tr", c, half)] = tr
 
-        def X_in(c):
-            h1grp = work.tile([P, T, 4], BF16, name="h1grp", tag="h1grp", bufs=2, align_bytes=64)
-            st[("h1grp", c)] = h1grp
-            g32 = h1grp[:].bitcast(F32)
-            for half in range(2):
-                copy_out(
-                    "v" if (c == 0 and half == 1) else X_ENG[half],
-                    g32[:, 256 * half : 256 * half + 256, :],
-                    st[("tr", c, half)][:].rearrange("p u w -> p w u"),
+        def X_in(c, half, on_vector):
+            if ("h1grp", c) not in st:
+                st[("h1grp", c)] = work.tile(
+                    [P, T, 4], BF16, name="h1grp", tag="h1grp", bufs=2, align_bytes=64
                 )
+            dst = st[("h1grp", c)][:].bitcast(F32)[:, 256 * half : 256 * half + 256, :]
+            src = st[("tr", c, half)][:].rearrange("p u w -> p w u")
+            if on_vector:
+                nc.vector.tensor_copy(out=dst, in_=src)
+            else:
+                nc.scalar.copy(out=dst, in_=src)
 
         def Q1(c):
             h1c = work.tile([P, T], U32, name="h1c", tag="h1c", bufs=2, align_bytes=64)
@@ -191,10 +184,10 @@ def tile_cfccell_pa_t_kernel(
             )
             st[("h1c", c)] = (h1c, h1s)
 
-        def P1(c, g, j):
+        def P1(c, n):
             h1c, h1s = st[("h1c", c)]
-            acc = psum.tile([P, T], F32, name="s1", tag="mm", bufs=5)
-            cols = slice(P * (4 * g + j), P * (4 * g + j) + P)
+            acc = psum.tile([P, T], F32, name="s1", tag="s1", bufs=3)
+            cols = slice(P * n, P * n + P)
             nc.tensor.matmul_mx(
                 out=acc[:],
                 lhsT=w1c[:, cols].bitcast(FP8X4),
@@ -204,16 +197,17 @@ def tile_cfccell_pa_t_kernel(
                 start=True,
                 stop=True,
             )
-            st[("s1", c, g, j)] = acc
+            st[("s1", c, n)] = acc
 
-        def A1(c, g, j):
+        def A1(c, n):
+            g, j = n // 4, n % 4
             if j == 0:
                 st[("th1", c, g)] = work.tile([P, 4, T], F32, name="th1", tag="th1", bufs=3)
             nc.scalar.activation(
                 out=st[("th1", c, g)][:, j, :],
-                in_=st[("s1", c, g, j)][:],
+                in_=st[("s1", c, n)][:],
                 func=AF.Tanh,
-                bias=b1s[:, 4 * g + j : 4 * g + j + 1],
+                bias=b1s[:, n : n + 1],
                 scale=LECUN_B,
             )
 
@@ -229,8 +223,8 @@ def tile_cfccell_pa_t_kernel(
             st[("xgrp", c, g)] = xgrp
 
         def Q2(c, g):
-            xc = work.tile([P, T], U32, name="xc", tag="xc%d" % g, bufs=4, align_bytes=64)
-            xs = work.tile([P, T], U8, name="xs", tag="xs%d" % g, bufs=4, align_bytes=64)
+            xc = work.tile([P, T], U32, name="xc", tag="xc%d" % g, bufs=3, align_bytes=64)
+            xs = work.tile([P, T], U8, name="xs", tag="xs%d" % g, bufs=3, align_bytes=64)
             nc.vector.quantize_mx(
                 out=xc[:].bitcast(FP8X4),
                 scales=xs[:],
@@ -239,7 +233,7 @@ def tile_cfccell_pa_t_kernel(
             st[("xc", c, g)] = (xc, xs)
 
         def S2(c, k):
-            acc = psum.tile([P, T], F32, name="s2", tag="mm", bufs=5)
+            acc = psum.tile([P, T], F32, name="s2", tag="s2", bufs=2)
             for g in range(2):
                 xc, xs = st[("xc", c, g)]
                 cols = slice(P * (2 * k + g), P * (2 * k + g) + P)
@@ -255,7 +249,7 @@ def tile_cfccell_pa_t_kernel(
             st[("s2", c, k)] = acc
 
         def FF(c, k):
-            ff = work.tile([P, T], F32, name="ff", tag="ff%d" % k, bufs=3)
+            ff = work.tile([P, T], F32, name="ff", tag="ff%d" % k, bufs=2)
             nc.scalar.activation(
                 out=ff[:], in_=st[("s2", c, k)][:], func=AF.Tanh, bias=bh[:, k : k + 1],
                 scale=(-1.0 if k == 0 else 1.0),
@@ -264,137 +258,148 @@ def tile_cfccell_pa_t_kernel(
 
         def Ea(c):
             u = work.tile([P, T], F32, name="u", tag="u", bufs=2)
+            cols = slice(T * (c % 4), T * (c % 4) + T)
             nc.vector.scalar_tensor_tensor(
-                out=u[:].rearrange("q (r p) -> q r p", r=4),
-                in0=st[("s2", c, 2)][:].rearrange("q (r p) -> q r p", r=4),
+                out=u[:].rearrange("q (r p) -> q r p", r=R),
+                in0=st[("s2", c, 2)][:].rearrange("q (r p) -> q r p", r=R),
                 scalar=bh[:, 2:3],
-                in1=ts_bc[:, T * c : T * c + T].rearrange("q (p r) -> q r p", r=4),
+                in1=ts_bc[c // 4][:, cols].rearrange("q (p r) -> q r p", r=R),
                 op0=ALU.add,
                 op1=ALU.mult,
             )
             st[("u", c)] = u
 
         def Eb(c):
-            v = work.tile([P, T], F32, name="v", tag="v", bufs=3)
-            nc.vector.tensor_tensor(out=v[:], in0=st[("u", c)][:], in1=st[("s2", c, 3)][:], op=ALU.add)
+            v = work.tile([P, T], F32, name="v", tag="v", bufs=2)
+            nc.vector.scalar_tensor_tensor(
+                out=v[:], in0=st[("u", c)][:], scalar=bh[:, 3:4], in1=st[("s2", c, 3)][:],
+                op0=ALU.add, op1=ALU.add,
+            )
             st[("v", c)] = v
 
-        def TH(c):
-            th = work.tile([P, T], F32, name="th", tag="th", bufs=3)
-            nc.scalar.activation(
-                out=th[:], in_=st[("v", c)][:], func=AF.Tanh, bias=bh[:, 3:4], scale=0.5
+        def turn(dst, src, start, stop):
+            nc.tensor.matmul(
+                out=dst, lhsT=src, rhs=ident[:], start=start, stop=stop, is_transpose=True
             )
+
+        def T_out(c):
+            v_t = psum.tile([P, R, H], F32, name="v_t", tag="tr", bufs=3)
+            d_t = psum.tile([P, R, H], F32, name="d_t", tag="tr", bufs=3)
+            n_t = psum.tile([P, R, H], F32, name="n_t", tag="tr", bufs=3)
+            for r in range(R):
+                turn(v_t[:, r, :], st[("v", c)][:, P * r : P * r + P], True, True)
+            for r in range(R):
+                turn(d_t[:, r, :], st[("ff", c, 0)][:, P * r : P * r + P], True, False)
+                turn(d_t[:, r, :], st[("ff", c, 1)][:, P * r : P * r + P], False, True)
+            for r in range(R):
+                turn(n_t[:, r, :], st[("ff", c, 0)][:, P * r : P * r + P], True, True)
+            st[("out", c)] = (v_t, d_t, n_t)
+
+        def TH(c):
+            th = work.tile([P, R, H], F32, name="th", tag="th", bufs=2)
+            nc.scalar.activation(out=th[:], in_=st[("out", c)][0][:], func=AF.Tanh, scale=0.5)
             st[("th", c)] = th
 
         def Em(c):
-            e1 = work.tile([P, T], F32, name="e1", tag="e1", bufs=2)
+            e = work.tile([P, R, H], F32, name="e", tag="e", bufs=2)
             nc.vector.scalar_tensor_tensor(
-                out=e1[:], in0=st[("th", c)][:], scalar=1.0, in1=st[("ff", c, 0)][:],
-                op0=ALU.subtract, op1=ALU.mult,
-            )
-            st[("e1", c)] = e1
-
-        def Eo(c):
-            e2 = work.tile([P, T], F32, name="e2", tag="e2", bufs=2)
-            nc.vector.scalar_tensor_tensor(
-                out=e2[:], in0=st[("th", c)][:], scalar=1.0, in1=st[("ff", c, 1)][:],
+                out=e[:], in0=st[("th", c)][:], scalar=1.0, in1=st[("out", c)][1][:],
                 op0=ALU.add, op1=ALU.mult,
             )
-            st[("e2", c)] = e2
+            st[("e", c)] = e
 
-        def TO(c):
-            tro = psum.tile([P, 4, H], F32, name="tro", tag="tr", bufs=3)
-            for r in range(4):
-                nc.tensor.matmul(
-                    out=tro[:, r, :], lhsT=st[("e1", c)][:, P * r : P * r + P], rhs=ident[:],
-                    start=True, stop=False, is_transpose=True,
-                )
-                nc.tensor.matmul(
-                    out=tro[:, r, :], lhsT=st[("e2", c)][:, P * r : P * r + P], rhs=ident[:],
-                    start=False, stop=True, is_transpose=True,
-                )
-            st[("tro", c)] = tro
-
-        def XO(c):
-            osb = work.tile([P, 4, H], F32, name="osb", tag="osb", bufs=3)
-            nc.scalar.mul(out=osb[:], in_=st[("tro", c)][:], mul=0.5)
-            nc.sync.dma_start(out=out[c].rearrange("(p r) h -> p r h", r=4), in_=osb[:])
+        def Eo(c):
+            osb = work.tile([P, R, H], F32, name="osb", tag="osb", bufs=3)
+            nc.vector.scalar_tensor_tensor(
+                out=osb[:], in0=st[("e", c)][:], scalar=0.5, in1=st[("out", c)][2][:],
+                op0=ALU.mult, op1=ALU.subtract,
+            )
+            nc.sync.dma_start(out=out[c].rearrange("(p r) h -> p r h", r=R), in_=osb[:])
 
         def ok(c):
             return 0 <= c < NB
 
-        LS, LT, LE, LO = 2, 3, 4, 5
-
         T_in(0)
-        X_in(0)
         b1_prep()
+        X_in(0, 0, False)
+        X_in(0, 1, False)
         w1_group(0)
-        Q1(0)
         w1_group(1)
         w1_quant(0)
-        for k in range(2, 8):
+        w1_group(2)
+        Q1(0)
+        w1_quant(1)
+        P1(0, 0)
+        P1(0, 1)
+        w1_group(3)
+        w1_quant(2)
+        P1(0, 2)
+        w1_quant(3)
+        for k in range(4, 8):
             w1_group(k)
-            w1_quant(k - 1)
-            if k < 5:
-                P1(0, 0, k - 2)
+            if k > 4:
+                w1_quant(k - 1)
         w1_quant(7)
 
-        for i in range(NB + LO):
-            c = i - LS
+        for i in range(NB + 2):
+            b, a = i - 1, i - 2
+            if ok(a):
+                T_out(a)
             if ok(i):
-                P1(i, 0, 3)
-            if ok(i - LO):
-                TO(i - LO)
+                A1(i, 0)
+                P1(i, 3)
+            if ok(a):
+                TH(a)
+            if ok(b):
+                M(b, 0)
+                M(b, 1)
+                Q2(b, 0)
+            if ok(a):
+                Em(a)
+            if ok(b):
+                Q2(b, 1)
+            if ok(a):
+                Eo(a)
             if ok(i + 1):
                 T_in(i + 1)
             if ok(i):
-                A1(i, 0, 0)
-            if ok(i - LE):
-                Em(i - LE)
-                Eo(i - LE)
-            if ok(i - 1):
-                Q2(i - 1, 1)
-            if ok(c):
-                S2(c, 2)
-                S2(c, 3)
+                A1(i, 1)
+                P1(i, 4)
+            if ok(b):
+                S2(b, 2)
             if ok(i):
-                for j in range(3):
-                    A1(i, 0, j + 1)
-                    P1(i, 1, j)
-            if ok(c):
-                Ea(c)
-                Eb(c)
-            if ok(i - LO):
-                XO(i - LO)
-            if ok(i - LT):
-                TH(i - LT)
-            if ok(i + 1):
-                X_in(i + 1)
+                A1(i, 2)
+                P1(i, 5)
+            if ok(b):
+                S2(b, 3)
             if ok(i):
-                M(i, 0)
-            if ok(i + 1):
-                Q1(i + 1)
-            if ok(i):
-                Q2(i, 0)
-            if i < 2:
-                wh_group(i)
+                A1(i, 3)
+                P1(i, 6)
             if i == 0:
                 bias_prep()
-            if ok(i):
-                A1(i, 1, 0)
-                P1(i, 1, 3)
-            if ok(c):
-                S2(c, 0)
-                S2(c, 1)
-            if ok(i):
-                for j in range(3):
-                    A1(i, 1, j + 1)
-                    if ok(i + 1):
-                        P1(i + 1, 0, j)
-            if ok(c):
-                FF(c, 0)
-                FF(c, 1)
-            if ok(i):
-                M(i, 1)
             if i < 2:
-                wh_quant(i)
+                wh_group(1 - i)
+            if ok(i + 1):
+                X_in(i + 1, 0, False)
+                X_in(i + 1, 1, True)
+            if ok(i):
+                A1(i, 4)
+                P1(i, 7)
+            if ok(b):
+                Ea(b)
+            if i < 2:
+                wh_quant(1 - i)
+            if ok(b):
+                Eb(b)
+                S2(b, 0)
+                S2(b, 1)
+            if ok(i + 1):
+                Q1(i + 1)
+            for n in range(3):
+                if ok(i):
+                    A1(i, 5 + n)
+                if ok(i + 1):
+                    P1(i + 1, n)
+            if ok(b):
+                FF(b, 0)
+                FF(b, 1)

@@ -232,8 +232,8 @@ def tile_cfccell_pa_t_kernel(
             )
             st[("xc", c, g)] = (xc, xs)
 
-        def S2(c, k):
-            acc = psum.tile([P, T], F32, name="s2", tag="s2", bufs=2)
+        def S2(c, k, tag="s2", bufs=2):
+            acc = psum.tile([P, T], F32, name="s2", tag=tag, bufs=bufs)
             for g in range(2):
                 xc, xs = st[("xc", c, g)]
                 cols = slice(P * (2 * k + g), P * (2 * k + g) + P)
@@ -341,13 +341,12 @@ def tile_cfccell_pa_t_kernel(
                 w1_quant(k - 1)
         w1_quant(7)
 
-        for i in range(NB + 2):
+        for i in range(NB):
             b, a = i - 1, i - 2
             if ok(a):
                 T_out(a)
-            if ok(i):
-                A1(i, 0)
-                P1(i, 3)
+            A1(i, 0)
+            P1(i, 3)
             if ok(a):
                 TH(a)
             if ok(b):
@@ -362,29 +361,25 @@ def tile_cfccell_pa_t_kernel(
                 Eo(a)
             if ok(i + 1):
                 T_in(i + 1)
-            if ok(i):
-                A1(i, 1)
-                P1(i, 4)
+            A1(i, 1)
+            P1(i, 4)
             if ok(b):
                 S2(b, 2)
-            if ok(i):
-                A1(i, 2)
-                P1(i, 5)
+            A1(i, 2)
+            P1(i, 5)
             if ok(b):
                 S2(b, 3)
-            if ok(i):
-                A1(i, 3)
-                P1(i, 6)
-            if i == 0:
+            A1(i, 3)
+            P1(i, 6)
+            if i == 1:
                 bias_prep()
             if i < 2:
                 wh_group(1 - i)
             if ok(i + 1):
                 X_in(i + 1, 0, False)
-                X_in(i + 1, 1, True)
-            if ok(i):
-                A1(i, 4)
-                P1(i, 7)
+                X_in(i + 1, 1, i >= 2)
+            A1(i, 4)
+            P1(i, 7)
             if ok(b):
                 Ea(b)
             if i < 2:
@@ -396,10 +391,31 @@ def tile_cfccell_pa_t_kernel(
             if ok(i + 1):
                 Q1(i + 1)
             for n in range(3):
-                if ok(i):
-                    A1(i, 5 + n)
+                A1(i, 5 + n)
                 if ok(i + 1):
                     P1(i + 1, n)
             if ok(b):
                 FF(b, 0)
                 FF(b, 1)
+
+        a, b = NB - 2, NB - 1
+        M(b, 0)
+        T_out(a)
+        TH(a)
+        M(b, 1)
+        Q2(b, 0)
+        Q2(b, 1)
+        S2(b, 2)
+        S2(b, 3)
+        Em(a)
+        S2(b, 0, "s1", 3)
+        S2(b, 1, "s1", 3)
+        Ea(b)
+        Eo(a)
+        FF(b, 0)
+        FF(b, 1)
+        Eb(b)
+        T_out(b)
+        TH(b)
+        Em(b)
+        Eo(b)

@@ -16,6 +16,7 @@ ALU = mybir.AluOpType
 P = 128
 NB, T, U, V, H = 8, 512, 512, 1024, 128
 R = T // P
+V0 = 3
 LECUN_A = 1.7159
 LECUN_B = 0.666
 FLOPS = 2 * NB * T * U * V + 2 * NB * T * V * 4 * H
@@ -31,7 +32,12 @@ def tile_cfccell_pa_t_kernel(
         psum = ctx.enter_context(tc.psum_pool(name="psum", bufs=1))
         ctx.enter_context(tc.manual_schedule())
 
-        h1raw = [const.tile([P, R, U], BF16, name="h1raw%d" % c) for c in range(NB)]
+        h1raw = [const.tile([P, R, U], BF16, name="h1raw%d" % c) for c in range(V0)]
+        h1raw += [const.tile([P, 2, U], BF16, name="h1raw%d" % c) for c in range(V0, NB)]
+        h1vec = {
+            c: const.tile([P, 2 * U], BF16, name="h1vec%d" % c, align_bytes=64)
+            for c in range(V0, NB)
+        }
         w1raw = [const.tile([P, 4, V // 2], BF16, name="w1raw%d" % g) for g in range(2)]
         whraw = [const.tile([P, 2, 8, H], BF16, name="whraw%d" % p) for p in range(2)]
         ts_bc = [const.tile([P, 4 * T], BF16, name="ts_bc%d" % q) for q in range(2)]
@@ -43,8 +49,20 @@ def tile_cfccell_pa_t_kernel(
         def load_h1(c, r0, r1):
             nc.sync.dma_start(
                 out=h1raw[c][:, r0:r1, :],
-                in_=h1[c].rearrange("(p r) k -> p r k", r=R)[:, r0:r1, :],
+                in_=h1[c].rearrange("(r p) k -> p r k", p=P)[:, r0:r1, :],
             )
+
+        def load_h1_both(c):
+            if c < V0:
+                load_h1(c, 0, 4)
+                return
+            load_h1(c, 0, 2)
+            pieces = h1[c][T // 2 : T, :].rearrange("(b t) (u a j) -> a (t u) b j", b=16, u=2, a=4)
+            for a in range(4):
+                nc.sync.dma_start(
+                    out=h1vec[c][32 * a : 32 * a + 32, :].rearrange("q (b j) -> q b j", b=16),
+                    in_=pieces[a],
+                )
 
         def load_w1(g):
             for u in range(2):
@@ -74,16 +92,12 @@ def tile_cfccell_pa_t_kernel(
         load_h1(0, 2, 4)
         load_w1(0)
         load_w1(1)
-        load_h1(1, 0, 4)
+        load_h1_both(1)
         load_wh(1)
-        load_h1(2, 0, 4)
+        load_h1_both(2)
         load_wh(0)
         load_ts(0)
-        load_h1(3, 0, 4)
-        load_h1(4, 0, 4)
-        load_ts(1)
-        for c in range(5, NB):
-            load_h1(c, 0, 4)
+        load_h1_both(3)
 
         ident = const.tile([P, P], F32, name="ident")
         make_identity(nc, ident[:])
@@ -151,7 +165,7 @@ def tile_cfccell_pa_t_kernel(
 
         def T_in(c):
             words = h1raw[c][:].bitcast(F32)
-            for half in range(2):
+            for half in range(2 if c < V0 else 1):
                 tr = psum.tile([P, 2, 256], F32, name="tr", tag="tr", bufs=3)
                 for rr in range(2):
                     for u in range(2):
@@ -162,17 +176,22 @@ def tile_cfccell_pa_t_kernel(
                         )
                 st[("tr", c, half)] = tr
 
+        def new_grp(c):
+            st[("h1grp", c)] = work.tile(
+                [P, T, 4], BF16, name="h1grp", tag="h1grp", bufs=2, align_bytes=64
+            )
+
         def X_in(c, half, on_vector):
-            if ("h1grp", c) not in st:
-                st[("h1grp", c)] = work.tile(
-                    [P, T, 4], BF16, name="h1grp", tag="h1grp", bufs=2, align_bytes=64
-                )
             dst = st[("h1grp", c)][:].bitcast(F32)[:, 256 * half : 256 * half + 256, :]
             src = st[("tr", c, half)][:].rearrange("p u w -> p w u")
             if on_vector:
                 nc.vector.tensor_copy(out=dst, in_=src)
             else:
                 nc.scalar.copy(out=dst, in_=src)
+
+        def V_in(c):
+            dst = st[("h1grp", c)][:].bitcast(F32)[:, 256:512, :].rearrange("p w u -> p (w u)")
+            nc.vector.transpose(dst, h1vec[c][:].bitcast(F32))
 
         def Q1(c):
             h1c = work.tile([P, T], U32, name="h1c", tag="h1c", bufs=2, align_bytes=64)
@@ -260,10 +279,10 @@ def tile_cfccell_pa_t_kernel(
             u = work.tile([P, T], F32, name="u", tag="u", bufs=2)
             cols = slice(T * (c % 4), T * (c % 4) + T)
             nc.vector.scalar_tensor_tensor(
-                out=u[:].rearrange("q (r p) -> q r p", r=R),
-                in0=st[("s2", c, 2)][:].rearrange("q (r p) -> q r p", r=R),
+                out=u[:],
+                in0=st[("s2", c, 2)][:],
                 scalar=bh[:, 2:3],
-                in1=ts_bc[c // 4][:, cols].rearrange("q (p r) -> q r p", r=R),
+                in1=ts_bc[c // 4][:, cols],
                 op0=ALU.add,
                 op1=ALU.mult,
             )
@@ -314,13 +333,14 @@ def tile_cfccell_pa_t_kernel(
                 out=osb[:], in0=st[("e", c)][:], scalar=0.5, in1=st[("out", c)][2][:],
                 op0=ALU.mult, op1=ALU.subtract,
             )
-            nc.sync.dma_start(out=out[c].rearrange("(p r) h -> p r h", r=R), in_=osb[:])
+            nc.sync.dma_start(out=out[c].rearrange("(r p) h -> p r h", p=P), in_=osb[:])
 
         def ok(c):
             return 0 <= c < NB
 
         T_in(0)
         b1_prep()
+        new_grp(0)
         X_in(0, 0, False)
         X_in(0, 1, False)
         w1_group(0)
@@ -343,26 +363,25 @@ def tile_cfccell_pa_t_kernel(
 
         for i in range(NB):
             b, a = i - 1, i - 2
+            if ok(i + 4):
+                load_h1_both(i + 4)
+            if i == 0:
+                load_ts(1)
             if ok(a):
                 T_out(a)
             A1(i, 0)
             P1(i, 3)
-            if ok(a):
-                TH(a)
             if ok(b):
                 M(b, 0)
                 M(b, 1)
                 Q2(b, 0)
-            if ok(a):
-                Em(a)
-            if ok(b):
                 Q2(b, 1)
-            if ok(a):
-                Eo(a)
-            if ok(i + 1):
-                T_in(i + 1)
             A1(i, 1)
             P1(i, 4)
+            if ok(a):
+                TH(a)
+            if ok(i + 1):
+                T_in(i + 1)
             if ok(b):
                 S2(b, 2)
             A1(i, 2)
@@ -371,25 +390,33 @@ def tile_cfccell_pa_t_kernel(
                 S2(b, 3)
             A1(i, 3)
             P1(i, 6)
+            if ok(a):
+                Em(a)
             if i == 1:
                 bias_prep()
             if i < 2:
                 wh_group(1 - i)
             if ok(i + 1):
+                new_grp(i + 1)
                 X_in(i + 1, 0, False)
-                X_in(i + 1, 1, i >= 2)
+                if i + 1 < V0:
+                    X_in(i + 1, 1, False)
+                else:
+                    V_in(i + 1)
+            if ok(a):
+                Eo(a)
             A1(i, 4)
             P1(i, 7)
             if ok(b):
                 Ea(b)
             if i < 2:
                 wh_quant(1 - i)
+            if ok(i + 1):
+                Q1(i + 1)
             if ok(b):
                 Eb(b)
                 S2(b, 0)
                 S2(b, 1)
-            if ok(i + 1):
-                Q1(i + 1)
             for n in range(3):
                 A1(i, 5 + n)
                 if ok(i + 1):

@@ -16,6 +16,8 @@ ALU = mybir.AluOpType
 P = 128
 NB, T, U, V, H = 8, 512, 512, 1024, 128
 R = T // P
+WHOLE = [(c, 0, T) for c in range(NB - 1)]
+HALVES = [(NB - 1, 0, T // 2), (NB - 1, T // 2, T)]
 V0 = 3
 LECUN_A = 1.7159
 LECUN_B = 0.666
@@ -38,8 +40,8 @@ def tile_cfccell_pa_t_kernel(
             c: const.tile([P, 2 * U], BF16, name="h1vec%d" % c, align_bytes=64)
             for c in range(V0, NB)
         }
-        w1raw = [const.tile([P, 4, V // 2], BF16, name="w1raw%d" % g) for g in range(2)]
-        whraw = [const.tile([P, 2, 8, H], BF16, name="whraw%d" % p) for p in range(2)]
+        w1raw = [const.tile([P, 4, V // 4], BF16, name="w1raw%d" % g) for g in range(4)]
+        whraw = [const.tile([P, 8, H], BF16, name="whraw%d" % k) for k in range(4)]
         ts_bc = [const.tile([P, 4 * T], BF16, name="ts_bc%d" % q) for q in range(2)]
         b1raw = const.tile([P, 8], BF16, name="b1raw")
         bhraw = [const.tile([P, 1], BF16, name="bhraw%d" % k) for k in range(4)]
@@ -68,17 +70,13 @@ def tile_cfccell_pa_t_kernel(
             for u in range(2):
                 nc.sync.dma_start(
                     out=w1raw[g][:, 2 * u : 2 * u + 2, :],
-                    in_=W1[256 * u : 256 * u + 256, 512 * g : 512 * g + 512].rearrange(
+                    in_=W1[256 * u : 256 * u + 256, 256 * g : 256 * g + 256].rearrange(
                         "(p e) v -> p e v", e=2
                     ),
                 )
 
-        def load_wh(pair):
-            for k in range(2):
-                nc.sync.dma_start(
-                    out=whraw[pair][:, k, :, :],
-                    in_=heads[2 * pair + k].rearrange("(a q) n -> q a n", q=P),
-                )
+        def load_wh(k):
+            nc.sync.dma_start(out=whraw[k][:], in_=heads[k].rearrange("(a q) n -> q a n", q=P))
 
         def load_ts(q):
             nc.sync.dma_start(
@@ -86,16 +84,20 @@ def tile_cfccell_pa_t_kernel(
                 in_=ts_flat[4 * T * q : 4 * T * q + 4 * T].partition_broadcast(P),
             )
 
-        with nc.allow_non_contiguous_dma(reason="b1, one element of each 128 to a partition"):
-            nc.scalar.dma_start(out=b1raw[:], in_=b1.rearrange("(a q) -> q a", q=P))
         load_h1(0, 0, 2)
         load_h1(0, 2, 4)
         load_w1(0)
         load_w1(1)
+        with nc.allow_non_contiguous_dma(reason="b1, one element of each 128 to a partition"):
+            nc.sync.dma_start(out=b1raw[:], in_=b1.rearrange("(a q) -> q a", q=P))
+        load_w1(2)
+        load_w1(3)
+        load_wh(2)
         load_h1_both(1)
-        load_wh(1)
+        load_wh(3)
         load_h1_both(2)
         load_wh(0)
+        load_wh(1)
         load_ts(0)
         load_h1_both(3)
 
@@ -109,6 +111,16 @@ def tile_cfccell_pa_t_kernel(
         warm2 = const.tile([P, 1], F32, name="warm2")
         nc.scalar.activation(out=warm2[:], in_=warm[:], func=AF.Tanh)
 
+        zeros = const.tile([P, T], BF16, name="zeros")
+        nc.vector.memset(zeros[:], 0.0)
+
+        def keep_busy(count):
+            for n in range(count):
+                idle = psum.tile([P, T], F32, name="idle", tag="s1", bufs=3)
+                nc.tensor.matmul(
+                    out=idle[:], lhsT=zeros[:, 0:P], rhs=zeros[:], start=True, stop=True
+                )
+
         w1grp = const.tile([P, V, 4], BF16, name="w1grp", align_bytes=64)
         w1c = const.tile([P, V], U32, name="w1c", align_bytes=64)
         w1s = const.tile([P, V], U8, name="w1s", align_bytes=64)
@@ -118,14 +130,16 @@ def tile_cfccell_pa_t_kernel(
         b1s = const.tile([P, 8], F32, name="b1s")
         bh = const.tile([P, 4], F32, name="bh")
 
-        def w1_group(k):
+        def w1_group(k, on_vector=True):
             cols = slice(P * k, P * k + P)
-            nc.vector.tensor_copy(
-                out=w1grp[:, cols, :].rearrange("p (c i) t -> p c t i", i=4),
-                in_=w1raw[k // 4][:, :, P * (k % 4) : P * (k % 4) + P].rearrange(
-                    "p t (c i) -> p c t i", i=4
-                ),
+            dst = w1grp[:, cols, :].rearrange("p (c i) t -> p c t i", i=4)
+            src = w1raw[k // 2][:, :, P * (k % 2) : P * (k % 2) + P].rearrange(
+                "p t (c i) -> p c t i", i=4
             )
+            if on_vector:
+                nc.vector.tensor_copy(out=dst, in_=src)
+            else:
+                nc.scalar.copy(out=dst, in_=src)
 
         def w1_quant(k):
             cols = slice(P * k, P * k + P)
@@ -135,10 +149,10 @@ def tile_cfccell_pa_t_kernel(
                 in_=w1grp[:, cols, :].rearrange("p v t -> p (v t)"),
             )
 
-        def wh_group(pair):
+        def wh_group(k):
             nc.vector.tensor_copy(
-                out=whgrp[:, 4 * pair : 4 * pair + 4, :, :],
-                in_=whraw[pair][:].rearrange("p k (g j) n -> p (k g) n j", j=4),
+                out=whgrp[:, 2 * k : 2 * k + 2, :, :],
+                in_=whraw[k][:].rearrange("p (g j) n -> p g n j", j=4),
             )
 
         def wh_quant(pair):
@@ -203,58 +217,59 @@ def tile_cfccell_pa_t_kernel(
             )
             st[("h1c", c)] = (h1c, h1s)
 
-        def P1(c, n):
+        def P1(q, n):
+            c, lo, hi = q
             h1c, h1s = st[("h1c", c)]
-            acc = psum.tile([P, T], F32, name="s1", tag="s1", bufs=3)
+            acc = psum.tile([P, hi - lo], F32, name="s1", tag="s1", bufs=3)
             cols = slice(P * n, P * n + P)
             nc.tensor.matmul_mx(
                 out=acc[:],
                 lhsT=w1c[:, cols].bitcast(FP8X4),
                 lhsT_scale=w1s[:, cols],
-                rhs=h1c[:].bitcast(FP8X4),
-                rhs_scale=h1s[:],
+                rhs=h1c[:, lo:hi].bitcast(FP8X4),
+                rhs_scale=h1s[:, lo:hi],
                 start=True,
                 stop=True,
             )
-            st[("s1", c, n)] = acc
+            st[("s1", q, n)] = acc
 
-        def A1(c, n):
+        def A1(q, n):
             g, j = n // 4, n % 4
             if j == 0:
-                st[("th1", c, g)] = work.tile([P, 4, T], F32, name="th1", tag="th1", bufs=3)
+                st[("th1", q, g)] = work.tile([P, 4, q[2] - q[1]], F32, name="th1", tag="th1", bufs=4)
             nc.scalar.activation(
-                out=st[("th1", c, g)][:, j, :],
-                in_=st[("s1", c, n)][:],
+                out=st[("th1", q, g)][:, j, :],
+                in_=st[("s1", q, n)][:],
                 func=AF.Tanh,
                 bias=b1s[:, n : n + 1],
                 scale=LECUN_B,
             )
 
-        def M(c, g):
-            xgrp = work.tile([P, T, 4], BF16, name="xgrp", tag="xgrp", bufs=3, align_bytes=64)
+        def M(q, g):
+            xgrp = work.tile([P, q[2] - q[1], 4], BF16, name="xgrp", tag="xgrp", bufs=3, align_bytes=64)
             nc.vector.tensor_scalar(
                 out=xgrp[:].rearrange("p (c i) j -> p c j i", i=4),
-                in0=st[("th1", c, g)][:].rearrange("p j (c i) -> p c j i", i=4),
+                in0=st[("th1", q, g)][:].rearrange("p j (c i) -> p c j i", i=4),
                 scalar1=LECUN_A,
                 scalar2=None,
                 op0=ALU.mult,
             )
-            st[("xgrp", c, g)] = xgrp
+            st[("xgrp", q, g)] = xgrp
 
-        def Q2(c, g):
-            xc = work.tile([P, T], U32, name="xc", tag="xc%d" % g, bufs=3, align_bytes=64)
-            xs = work.tile([P, T], U8, name="xs", tag="xs%d" % g, bufs=3, align_bytes=64)
+        def Q2(q, g):
+            xc = work.tile([P, q[2] - q[1]], U32, name="xc", tag="xc%d" % g, bufs=3, align_bytes=64)
+            xs = work.tile([P, q[2] - q[1]], U8, name="xs", tag="xs%d" % g, bufs=3, align_bytes=64)
             nc.vector.quantize_mx(
                 out=xc[:].bitcast(FP8X4),
                 scales=xs[:],
-                in_=st[("xgrp", c, g)][:].rearrange("p w t -> p (w t)"),
+                in_=st[("xgrp", q, g)][:].rearrange("p w t -> p (w t)"),
             )
-            st[("xc", c, g)] = (xc, xs)
+            st[("xc", q, g)] = (xc, xs)
 
-        def S2(c, k, tag="s2", bufs=2):
-            acc = psum.tile([P, T], F32, name="s2", tag=tag, bufs=bufs)
+        def S2(q, k, tag="s2", bufs=2):
+            acc = psum.tile([P, q[2] - q[1]], F32, name="s2", tag=tag, bufs=bufs)
             for g in range(2):
-                xc, xs = st[("xc", c, g)]
+                xc, xs = st[("xc", q, g)]
                 cols = slice(P * (2 * k + g), P * (2 * k + g) + P)
                 nc.tensor.matmul_mx(
                     out=acc[:],
@@ -265,137 +280,145 @@ def tile_cfccell_pa_t_kernel(
                     start=(g == 0),
                     stop=(g == 1),
                 )
-            st[("s2", c, k)] = acc
+            st[("s2", q, k)] = acc
 
-        def FF(c, k):
-            ff = work.tile([P, T], F32, name="ff", tag="ff%d" % k, bufs=2)
+        def FF(q, k):
+            ff = work.tile([P, q[2] - q[1]], F32, name="ff", tag="ff%d" % k, bufs=2)
             nc.scalar.activation(
-                out=ff[:], in_=st[("s2", c, k)][:], func=AF.Tanh, bias=bh[:, k : k + 1],
+                out=ff[:], in_=st[("s2", q, k)][:], func=AF.Tanh, bias=bh[:, k : k + 1],
                 scale=(-1.0 if k == 0 else 1.0),
             )
-            st[("ff", c, k)] = ff
+            st[("ff", q, k)] = ff
 
-        def Ea(c):
-            u = work.tile([P, T], F32, name="u", tag="u", bufs=2)
-            cols = slice(T * (c % 4), T * (c % 4) + T)
+        def Ea(q):
+            u = work.tile([P, q[2] - q[1]], F32, name="u", tag="u", bufs=2)
+            c, lo, hi = q
+            t0 = T * (c % 4)
             nc.vector.scalar_tensor_tensor(
                 out=u[:],
-                in0=st[("s2", c, 2)][:],
+                in0=st[("s2", q, 2)][:],
                 scalar=bh[:, 2:3],
-                in1=ts_bc[c // 4][:, cols],
+                in1=ts_bc[c // 4][:, t0 + lo : t0 + hi],
                 op0=ALU.add,
                 op1=ALU.mult,
             )
-            st[("u", c)] = u
+            st[("u", q)] = u
 
-        def Eb(c):
-            v = work.tile([P, T], F32, name="v", tag="v", bufs=2)
+        def Eb(q):
+            v = work.tile([P, q[2] - q[1]], F32, name="v", tag="v", bufs=2)
             nc.vector.scalar_tensor_tensor(
-                out=v[:], in0=st[("u", c)][:], scalar=bh[:, 3:4], in1=st[("s2", c, 3)][:],
+                out=v[:], in0=st[("u", q)][:], scalar=bh[:, 3:4], in1=st[("s2", q, 3)][:],
                 op0=ALU.add, op1=ALU.add,
             )
-            st[("v", c)] = v
+            st[("v", q)] = v
 
         def turn(dst, src, start, stop):
             nc.tensor.matmul(
                 out=dst, lhsT=src, rhs=ident[:], start=start, stop=stop, is_transpose=True
             )
 
-        def T_out(c):
-            v_t = psum.tile([P, R, H], F32, name="v_t", tag="tr", bufs=3)
-            d_t = psum.tile([P, R, H], F32, name="d_t", tag="tr", bufs=3)
-            n_t = psum.tile([P, R, H], F32, name="n_t", tag="tr", bufs=3)
-            for r in range(R):
-                turn(v_t[:, r, :], st[("v", c)][:, P * r : P * r + P], True, True)
-            for r in range(R):
-                turn(d_t[:, r, :], st[("ff", c, 0)][:, P * r : P * r + P], True, False)
-                turn(d_t[:, r, :], st[("ff", c, 1)][:, P * r : P * r + P], False, True)
-            for r in range(R):
-                turn(n_t[:, r, :], st[("ff", c, 0)][:, P * r : P * r + P], True, True)
-            st[("out", c)] = (v_t, d_t, n_t)
+        def T_out(q):
+            v_t = psum.tile([P, (q[2] - q[1]) // P, H], F32, name="v_t", tag="tr", bufs=3)
+            d_t = psum.tile([P, (q[2] - q[1]) // P, H], F32, name="d_t", tag="tr", bufs=3)
+            n_t = psum.tile([P, (q[2] - q[1]) // P, H], F32, name="n_t", tag="tr", bufs=3)
+            for r in range((q[2] - q[1]) // P):
+                turn(v_t[:, r, :], st[("v", q)][:, P * r : P * r + P], True, True)
+            for r in range((q[2] - q[1]) // P):
+                turn(d_t[:, r, :], st[("ff", q, 0)][:, P * r : P * r + P], True, False)
+                turn(d_t[:, r, :], st[("ff", q, 1)][:, P * r : P * r + P], False, True)
+            for r in range((q[2] - q[1]) // P):
+                turn(n_t[:, r, :], st[("ff", q, 0)][:, P * r : P * r + P], True, True)
+            st[("out", q)] = (v_t, d_t, n_t)
 
-        def TH(c):
-            th = work.tile([P, R, H], F32, name="th", tag="th", bufs=2)
-            nc.scalar.activation(out=th[:], in_=st[("out", c)][0][:], func=AF.Tanh, scale=0.5)
-            st[("th", c)] = th
+        def TH(q):
+            th = work.tile([P, (q[2] - q[1]) // P, H], F32, name="th", tag="th", bufs=2)
+            nc.scalar.activation(out=th[:], in_=st[("out", q)][0][:], func=AF.Tanh, scale=0.5)
+            st[("th", q)] = th
 
-        def Em(c):
-            e = work.tile([P, R, H], F32, name="e", tag="e", bufs=2)
+        def Em(q):
+            e = work.tile([P, (q[2] - q[1]) // P, H], F32, name="e", tag="e", bufs=2)
             nc.vector.scalar_tensor_tensor(
-                out=e[:], in0=st[("th", c)][:], scalar=1.0, in1=st[("out", c)][1][:],
+                out=e[:], in0=st[("th", q)][:], scalar=1.0, in1=st[("out", q)][1][:],
                 op0=ALU.add, op1=ALU.mult,
             )
-            st[("e", c)] = e
+            st[("e", q)] = e
 
-        def Eo(c):
-            osb = work.tile([P, R, H], F32, name="osb", tag="osb", bufs=3)
+        def Eo(q):
+            osb = work.tile([P, (q[2] - q[1]) // P, H], F32, name="osb", tag="osb", bufs=3)
             nc.vector.scalar_tensor_tensor(
-                out=osb[:], in0=st[("e", c)][:], scalar=0.5, in1=st[("out", c)][2][:],
+                out=osb[:], in0=st[("e", q)][:], scalar=0.5, in1=st[("out", q)][2][:],
                 op0=ALU.mult, op1=ALU.subtract,
             )
-            nc.sync.dma_start(out=out[c].rearrange("(r p) h -> p r h", p=P), in_=osb[:])
+            c, lo, hi = q
+            nc.sync.dma_start(out=out[c][lo:hi].rearrange("(r p) h -> p r h", p=P), in_=osb[:])
 
         def ok(c):
             return 0 <= c < NB
 
+        keep_busy(3)
         T_in(0)
-        b1_prep()
+        keep_busy(5)
         new_grp(0)
         X_in(0, 0, False)
         X_in(0, 1, False)
         w1_group(0)
         w1_group(1)
         w1_quant(0)
-        w1_group(2)
-        Q1(0)
         w1_quant(1)
-        P1(0, 0)
-        P1(0, 1)
-        w1_group(3)
+        Q1(0)
+        P1(WHOLE[0], 0)
+        P1(WHOLE[0], 1)
+        b1_prep()
+        w1_group(2, False)
+        w1_group(3, False)
         w1_quant(2)
-        P1(0, 2)
+        P1(WHOLE[0], 2)
         w1_quant(3)
-        for k in range(4, 8):
-            w1_group(k)
-            if k > 4:
-                w1_quant(k - 1)
+        w1_group(4)
+        w1_group(5)
+        w1_quant(4)
+        w1_group(6)
+        w1_quant(5)
+        w1_group(7)
+        w1_quant(6)
         w1_quant(7)
 
-        for i in range(NB):
-            b, a = i - 1, i - 2
+        for i in range(NB - 1):
+            q, b, a = WHOLE[i], i - 1, i - 2
             if ok(i + 4):
                 load_h1_both(i + 4)
             if i == 0:
                 load_ts(1)
             if ok(a):
-                T_out(a)
-            A1(i, 0)
-            P1(i, 3)
+                T_out(WHOLE[a])
+            A1(q, 0)
+            P1(q, 3)
             if ok(b):
-                M(b, 0)
-                M(b, 1)
-                Q2(b, 0)
-                Q2(b, 1)
-            A1(i, 1)
-            P1(i, 4)
+                M(WHOLE[b], 0)
+                M(WHOLE[b], 1)
+                Q2(WHOLE[b], 0)
+                Q2(WHOLE[b], 1)
+            A1(q, 1)
+            P1(q, 4)
             if ok(a):
-                TH(a)
+                TH(WHOLE[a])
             if ok(i + 1):
                 T_in(i + 1)
             if ok(b):
-                S2(b, 2)
-            A1(i, 2)
-            P1(i, 5)
+                S2(WHOLE[b], 2)
+            A1(q, 2)
+            P1(q, 5)
             if ok(b):
-                S2(b, 3)
-            A1(i, 3)
-            P1(i, 6)
+                S2(WHOLE[b], 3)
+            A1(q, 3)
+            P1(q, 6)
             if ok(a):
-                Em(a)
+                Em(WHOLE[a])
             if i == 1:
                 bias_prep()
             if i < 2:
-                wh_group(1 - i)
+                wh_group(2 - 2 * i)
+                wh_group(3 - 2 * i)
             if ok(i + 1):
                 new_grp(i + 1)
                 X_in(i + 1, 0, False)
@@ -404,45 +427,107 @@ def tile_cfccell_pa_t_kernel(
                 else:
                     V_in(i + 1)
             if ok(a):
-                Eo(a)
-            A1(i, 4)
-            P1(i, 7)
+                Eo(WHOLE[a])
+            A1(q, 4)
+            P1(q, 7)
             if ok(b):
-                Ea(b)
+                Ea(WHOLE[b])
             if i < 2:
                 wh_quant(1 - i)
             if ok(i + 1):
                 Q1(i + 1)
             if ok(b):
-                Eb(b)
-                S2(b, 0)
-                S2(b, 1)
+                Eb(WHOLE[b])
+                S2(WHOLE[b], 0)
+                S2(WHOLE[b], 1)
             for n in range(3):
-                A1(i, 5 + n)
+                A1(q, 5 + n)
                 if ok(i + 1):
-                    P1(i + 1, n)
+                    P1((WHOLE + HALVES)[i + 1], n)
             if ok(b):
-                FF(b, 0)
-                FF(b, 1)
+                FF(WHOLE[b], 0)
+                FF(WHOLE[b], 1)
 
-        a, b = NB - 2, NB - 1
-        M(b, 0)
+        z, a = WHOLE[-2:]
+        x, y = HALVES
+        T_out(z)
+        A1(x, 0)
+        P1(x, 3)
+        M(a, 0)
+        M(a, 1)
+        Q2(a, 0)
+        Q2(a, 1)
+        A1(x, 1)
+        P1(x, 4)
+        A1(x, 2)
+        P1(x, 5)
+        TH(z)
+        S2(a, 2)
+        A1(x, 3)
+        P1(x, 6)
+        A1(x, 4)
+        P1(x, 7)
+        S2(a, 3)
+        Em(z)
+        A1(x, 5)
+        P1(y, 0)
+        M(x, 0)
+        A1(x, 6)
+        P1(y, 1)
+        Eo(z)
+        A1(x, 7)
+        P1(y, 2)
+        Ea(a)
+        A1(y, 0)
+        P1(y, 3)
+        A1(y, 1)
+        P1(y, 4)
+        S2(a, 0)
+        M(x, 1)
+        Eb(a)
+        A1(y, 2)
+        P1(y, 5)
+        A1(y, 3)
+        P1(y, 6)
+        Q2(x, 0)
+        A1(y, 4)
+        P1(y, 7)
+        S2(a, 1)
+        Q2(x, 1)
+        A1(y, 5)
+        A1(y, 6)
+        A1(y, 7)
+        S2(x, 2, "s1", 3)
+        S2(x, 3, "s1", 3)
+        M(y, 0)
+        FF(a, 0)
+        M(y, 1)
+        FF(a, 1)
+        Q2(y, 0)
         T_out(a)
         TH(a)
-        M(b, 1)
-        Q2(b, 0)
-        Q2(b, 1)
-        S2(b, 2)
-        S2(b, 3)
+        Ea(x)
+        Q2(y, 1)
+        S2(x, 0)
+        S2(x, 1)
+        S2(y, 2, "s1", 3)
+        S2(y, 3, "s1", 3)
+        Eb(x)
+        FF(x, 0)
+        FF(x, 1)
+        S2(y, 0)
+        S2(y, 1)
         Em(a)
-        S2(b, 0, "s1", 3)
-        S2(b, 1, "s1", 3)
-        Ea(b)
+        Ea(y)
         Eo(a)
-        FF(b, 0)
-        FF(b, 1)
-        Eb(b)
-        T_out(b)
-        TH(b)
-        Em(b)
-        Eo(b)
+        T_out(x)
+        TH(x)
+        Eb(y)
+        FF(y, 0)
+        FF(y, 1)
+        Em(x)
+        Eo(x)
+        T_out(y)
+        TH(y)
+        Em(y)
+        Eo(y)

@@ -19,6 +19,7 @@ R = T // P
 WHOLE = [(c, 0, T) for c in range(NB - 1)]
 HALVES = [(NB - 1, 0, T // 2), (NB - 1, T // 2, T)]
 V0 = 3
+TOKENS = ["(p r)"] * V0 + ["(r p)"] * (NB - V0)
 LECUN_A = 1.7159
 LECUN_B = 0.666
 FLOPS = 2 * NB * T * U * V + 2 * NB * T * V * 4 * H
@@ -40,8 +41,8 @@ def tile_cfccell_pa_t_kernel(
             c: const.tile([P, 2 * U], BF16, name="h1vec%d" % c, align_bytes=64)
             for c in range(V0, NB)
         }
-        w1raw = [const.tile([P, 4, V // 4], BF16, name="w1raw%d" % g) for g in range(4)]
-        whraw = [const.tile([P, 8, H], BF16, name="whraw%d" % k) for k in range(4)]
+        w1raw = [const.tile([P, 4, V // 2], BF16, name="w1raw%d" % g) for g in range(2)]
+        whraw = [const.tile([P, 2, 4, H], BF16, name="whraw%d" % k) for k in range(4)]
         ts_bc = [const.tile([P, 4 * T], BF16, name="ts_bc%d" % q) for q in range(2)]
         b1raw = const.tile([P, 8], BF16, name="b1raw")
         bhraw = [const.tile([P, 1], BF16, name="bhraw%d" % k) for k in range(4)]
@@ -51,7 +52,7 @@ def tile_cfccell_pa_t_kernel(
         def load_h1(c, r0, r1):
             nc.sync.dma_start(
                 out=h1raw[c][:, r0:r1, :],
-                in_=h1[c].rearrange("(r p) k -> p r k", p=P)[:, r0:r1, :],
+                in_=h1[c].rearrange(TOKENS[c] + " k -> p r k", p=P)[:, r0:r1, :],
             )
 
         def load_h1_both(c):
@@ -70,13 +71,15 @@ def tile_cfccell_pa_t_kernel(
             for u in range(2):
                 nc.sync.dma_start(
                     out=w1raw[g][:, 2 * u : 2 * u + 2, :],
-                    in_=W1[256 * u : 256 * u + 256, 256 * g : 256 * g + 256].rearrange(
+                    in_=W1[256 * u : 256 * u + 256, 512 * g : 512 * g + 512].rearrange(
                         "(p e) v -> p e v", e=2
                     ),
                 )
 
         def load_wh(k):
-            nc.sync.dma_start(out=whraw[k][:], in_=heads[k].rearrange("(a q) n -> q a n", q=P))
+            nc.sync.dma_start(
+                out=whraw[k][:], in_=heads[k].rearrange("(g q j) n -> q g j n", g=2, j=4)
+            )
 
         def load_ts(q):
             nc.sync.dma_start(
@@ -84,16 +87,17 @@ def tile_cfccell_pa_t_kernel(
                 in_=ts_flat[4 * T * q : 4 * T * q + 4 * T].partition_broadcast(P),
             )
 
+        load_w1(0)
         load_h1(0, 0, 2)
         load_h1(0, 2, 4)
-        load_w1(0)
+        with nc.allow_non_contiguous_dma(reason="b1, two runs of four elements to a partition"):
+            nc.sync.dma_start(
+                out=b1raw[:].rearrange("q (g j) -> q g j", g=2),
+                in_=b1.rearrange("(g q j) -> q g j", g=2, j=4),
+            )
         load_w1(1)
-        with nc.allow_non_contiguous_dma(reason="b1, one element of each 128 to a partition"):
-            nc.sync.dma_start(out=b1raw[:], in_=b1.rearrange("(a q) -> q a", q=P))
-        load_w1(2)
-        load_w1(3)
-        load_wh(2)
         load_h1_both(1)
+        load_wh(2)
         load_wh(3)
         load_h1_both(2)
         load_wh(0)
@@ -130,16 +134,11 @@ def tile_cfccell_pa_t_kernel(
         b1s = const.tile([P, 8], F32, name="b1s")
         bh = const.tile([P, 4], F32, name="bh")
 
-        def w1_group(k, on_vector=True):
-            cols = slice(P * k, P * k + P)
-            dst = w1grp[:, cols, :].rearrange("p (c i) t -> p c t i", i=4)
-            src = w1raw[k // 2][:, :, P * (k % 2) : P * (k % 2) + P].rearrange(
-                "p t (c i) -> p c t i", i=4
+        def w1_group(g):
+            nc.vector.tensor_copy(
+                out=w1grp[:, 512 * g : 512 * g + 512, :].rearrange("p (j q) t -> p q t j", j=4),
+                in_=w1raw[g][:].rearrange("p t (q j) -> p q t j", j=4),
             )
-            if on_vector:
-                nc.vector.tensor_copy(out=dst, in_=src)
-            else:
-                nc.scalar.copy(out=dst, in_=src)
 
         def w1_quant(k):
             cols = slice(P * k, P * k + P)
@@ -152,7 +151,7 @@ def tile_cfccell_pa_t_kernel(
         def wh_group(k):
             nc.vector.tensor_copy(
                 out=whgrp[:, 2 * k : 2 * k + 2, :, :],
-                in_=whraw[k][:].rearrange("p (g j) n -> p g n j", j=4),
+                in_=whraw[k][:].rearrange("p g j n -> p g n j"),
             )
 
         def wh_quant(pair):
@@ -295,10 +294,10 @@ def tile_cfccell_pa_t_kernel(
             c, lo, hi = q
             t0 = T * (c % 4)
             nc.vector.scalar_tensor_tensor(
-                out=u[:],
-                in0=st[("s2", q, 2)][:],
+                out=u[:].rearrange("h (r p) -> h r p", p=P),
+                in0=st[("s2", q, 2)][:].rearrange("h (r p) -> h r p", p=P),
                 scalar=bh[:, 2:3],
-                in1=ts_bc[c // 4][:, t0 + lo : t0 + hi],
+                in1=ts_bc[c // 4][:, t0 + lo : t0 + hi].rearrange("h " + TOKENS[c] + " -> h r p", p=P),
                 op0=ALU.add,
                 op1=ALU.mult,
             )
@@ -350,38 +349,27 @@ def tile_cfccell_pa_t_kernel(
                 op0=ALU.mult, op1=ALU.subtract,
             )
             c, lo, hi = q
-            nc.sync.dma_start(out=out[c][lo:hi].rearrange("(r p) h -> p r h", p=P), in_=osb[:])
+            nc.sync.dma_start(out=out[c][lo:hi].rearrange(TOKENS[c] + " h -> p r h", p=P), in_=osb[:])
 
         def ok(c):
             return 0 <= c < NB
 
-        keep_busy(3)
-        T_in(0)
         keep_busy(5)
+        w1_group(0)
+        for n in range(4):
+            w1_quant(n)
+        T_in(0)
+        keep_busy(4)
         new_grp(0)
         X_in(0, 0, False)
-        X_in(0, 1, False)
-        w1_group(0)
-        w1_group(1)
-        w1_quant(0)
-        w1_quant(1)
-        Q1(0)
-        P1(WHOLE[0], 0)
-        P1(WHOLE[0], 1)
+        X_in(0, 1, True)
         b1_prep()
-        w1_group(2, False)
-        w1_group(3, False)
-        w1_quant(2)
-        P1(WHOLE[0], 2)
-        w1_quant(3)
-        w1_group(4)
-        w1_group(5)
-        w1_quant(4)
-        w1_group(6)
-        w1_quant(5)
-        w1_group(7)
-        w1_quant(6)
-        w1_quant(7)
+        Q1(0)
+        for n in range(3):
+            P1(WHOLE[0], n)
+        w1_group(1)
+        for n in range(4, 8):
+            w1_quant(n)
 
         for i in range(NB - 1):
             q, b, a = WHOLE[i], i - 1, i - 2

@@ -134,11 +134,13 @@ def tile_cfccell_pa_t_kernel(
         b1s = const.tile([P, 8], F32, name="b1s")
         bh = const.tile([P, 4], F32, name="bh")
 
-        def w1_group(g):
-            nc.vector.tensor_copy(
-                out=w1grp[:, 512 * g : 512 * g + 512, :].rearrange("p (j q) t -> p q t j", j=4),
-                in_=w1raw[g][:].rearrange("p t (q j) -> p q t j", j=4),
-            )
+        def w1_group(n, on_vector):
+            dst = w1grp[:, P * n : P * n + P, :].rearrange("p (c i) t -> p c t i", i=4)
+            src = w1raw[n // 4][:].rearrange("p t (c i j) -> p j c t i", i=4, j=4)[:, n % 4]
+            if on_vector:
+                nc.vector.tensor_copy(out=dst, in_=src)
+            else:
+                nc.scalar.copy(out=dst, in_=src)
 
         def w1_quant(k):
             cols = slice(P * k, P * k + P)
@@ -355,19 +357,24 @@ def tile_cfccell_pa_t_kernel(
             return 0 <= c < NB
 
         keep_busy(5)
-        w1_group(0)
         for n in range(4):
-            w1_quant(n)
+            w1_group(n, True)
+            if n > 0:
+                w1_quant(n - 1)
         T_in(0)
         keep_busy(4)
         new_grp(0)
         X_in(0, 0, False)
         X_in(0, 1, True)
+        w1_quant(3)
         b1_prep()
         Q1(0)
         for n in range(3):
             P1(WHOLE[0], n)
-        w1_group(1)
+        w1_group(4, False)
+        w1_group(5, False)
+        w1_group(6, True)
+        w1_group(7, True)
         for n in range(4, 8):
             w1_quant(n)
 

@@ -371,6 +371,7 @@ def tile_cfccell_pa_t_kernel(
         Q1(0)
         for n in range(3):
             P1(WHOLE[0], n)
+        T_in(1)
         w1_group(4, False)
         w1_group(5, False)
         w1_group(6, True)
@@ -397,7 +398,7 @@ def tile_cfccell_pa_t_kernel(
             P1(q, 4)
             if ok(a):
                 TH(WHOLE[a])
-            if ok(i + 1):
+            if 1 <= i:
                 T_in(i + 1)
             if ok(b):
                 S2(WHOLE[b], 2)
@@ -418,7 +419,7 @@ def tile_cfccell_pa_t_kernel(
                 new_grp(i + 1)
                 X_in(i + 1, 0, False)
                 if i + 1 < V0:
-                    X_in(i + 1, 1, False)
+                    X_in(i + 1, 1, i == 0)
                 else:
                     V_in(i + 1)
             if ok(a):

@@ -125,14 +125,14 @@ def tile_cfccell_pa_t_kernel(
                     out=idle[:], lhsT=zeros[:, 0:P], rhs=zeros[:], start=True, stop=True
                 )
 
-        w1grp = const.tile([P, V, 4], BF16, name="w1grp", align_bytes=64)
-        w1c = const.tile([P, V], U32, name="w1c", align_bytes=64)
-        w1s = const.tile([P, V], U8, name="w1s", align_bytes=64)
-        whgrp = const.tile([P, 8, H, 4], BF16, name="whgrp", align_bytes=64)
-        whc = const.tile([P, 8 * H], U32, name="whc", align_bytes=64)
-        whs = const.tile([P, 8 * H], U8, name="whs", align_bytes=64)
+        w1grp = const.tile([P, V, 4], BF16, name="w1grp", align_bytes=256)
+        w1c = const.tile([P, V], U32, name="w1c", align_bytes=256)
+        w1s = const.tile([P, V], U8, name="w1s", align_bytes=256)
+        whgrp = const.tile([P, 8, H, 4], BF16, name="whgrp", align_bytes=256)
+        whc = const.tile([P, 8 * H], U32, name="whc", align_bytes=256)
+        whs = const.tile([P, 8 * H], U8, name="whs", align_bytes=256)
         b1s = const.tile([P, 8], F32, name="b1s")
-        bh = const.tile([P, 4], F32, name="bh")
+        nb_ff1 = const.tile([P, 1], F32, name="nb_ff1")
 
         def w1_group(n, on_vector):
             dst = w1grp[:, P * n : P * n + P, :].rearrange("p (c i) t -> p c t i", i=4)
@@ -142,8 +142,8 @@ def tile_cfccell_pa_t_kernel(
             else:
                 nc.scalar.copy(out=dst, in_=src)
 
-        def w1_quant(k):
-            cols = slice(P * k, P * k + P)
+        def w1_quant(n0, n1):
+            cols = slice(P * n0, P * n1)
             nc.vector.quantize_mx(
                 out=w1c[:, cols].bitcast(FP8X4),
                 scales=w1s[:, cols],
@@ -165,16 +165,11 @@ def tile_cfccell_pa_t_kernel(
             )
 
         def b1_prep():
-            nc.vector.tensor_scalar(
-                out=b1s[:], in0=b1raw[:], scalar1=LECUN_B, scalar2=None, op0=ALU.mult
-            )
+            nc.scalar.mul(out=b1s[:], in_=b1raw[:], mul=LECUN_B)
 
-        def bias_prep():
-            nc.vector.tensor_scalar(
-                out=bh[:, 0:1], in0=bhraw[0][:], scalar1=-1.0, scalar2=None, op0=ALU.mult
-            )
-            for k in range(1, 4):
-                nc.vector.tensor_copy(out=bh[:, k : k + 1], in_=bhraw[k][:])
+        nc.gpsimd.tensor_scalar(
+            out=nb_ff1[:], in0=bhraw[0][:], scalar1=-1.0, scalar2=0.0, op0=ALU.mult, op1=ALU.add
+        )
 
         st = {}
 
@@ -193,7 +188,7 @@ def tile_cfccell_pa_t_kernel(
 
         def new_grp(c):
             st[("h1grp", c)] = work.tile(
-                [P, T, 4], BF16, name="h1grp", tag="h1grp", bufs=2, align_bytes=64
+                [P, T, 4], BF16, name="h1grp", tag="h1grp", bufs=2, align_bytes=256
             )
 
         def X_in(c, half, on_vector):
@@ -209,8 +204,8 @@ def tile_cfccell_pa_t_kernel(
             nc.vector.transpose(dst, h1vec[c][:].bitcast(F32))
 
         def Q1(c):
-            h1c = work.tile([P, T], U32, name="h1c", tag="h1c", bufs=2, align_bytes=64)
-            h1s = work.tile([P, T], U8, name="h1s", tag="h1s", bufs=2, align_bytes=64)
+            h1c = work.tile([P, T], U32, name="h1c", tag="h1c", bufs=2, align_bytes=256)
+            h1s = work.tile([P, T], U8, name="h1s", tag="h1s", bufs=2, align_bytes=256)
             nc.vector.quantize_mx(
                 out=h1c[:].bitcast(FP8X4),
                 scales=h1s[:],
@@ -247,7 +242,7 @@ def tile_cfccell_pa_t_kernel(
             )
 
         def M(q, g):
-            xgrp = work.tile([P, q[2] - q[1], 4], BF16, name="xgrp", tag="xgrp", bufs=3, align_bytes=64)
+            xgrp = work.tile([P, q[2] - q[1], 4], BF16, name="xgrp", tag="xgrp", bufs=3, align_bytes=256)
             nc.vector.tensor_scalar(
                 out=xgrp[:].rearrange("p (c i) j -> p c j i", i=4),
                 in0=st[("th1", q, g)][:].rearrange("p j (c i) -> p c j i", i=4),
@@ -258,8 +253,8 @@ def tile_cfccell_pa_t_kernel(
             st[("xgrp", q, g)] = xgrp
 
         def Q2(q, g):
-            xc = work.tile([P, q[2] - q[1]], U32, name="xc", tag="xc%d" % g, bufs=3, align_bytes=64)
-            xs = work.tile([P, q[2] - q[1]], U8, name="xs", tag="xs%d" % g, bufs=3, align_bytes=64)
+            xc = work.tile([P, q[2] - q[1]], U32, name="xc", tag="xc%d" % g, bufs=3, align_bytes=256)
+            xs = work.tile([P, q[2] - q[1]], U8, name="xs", tag="xs%d" % g, bufs=3, align_bytes=256)
             nc.vector.quantize_mx(
                 out=xc[:].bitcast(FP8X4),
                 scales=xs[:],
@@ -286,7 +281,8 @@ def tile_cfccell_pa_t_kernel(
         def FF(q, k):
             ff = work.tile([P, q[2] - q[1]], F32, name="ff", tag="ff%d" % k, bufs=2)
             nc.scalar.activation(
-                out=ff[:], in_=st[("s2", q, k)][:], func=AF.Tanh, bias=bh[:, k : k + 1],
+                out=ff[:], in_=st[("s2", q, k)][:], func=AF.Tanh,
+                bias=(nb_ff1 if k == 0 else bhraw[1])[:],
                 scale=(-1.0 if k == 0 else 1.0),
             )
             st[("ff", q, k)] = ff
@@ -298,7 +294,7 @@ def tile_cfccell_pa_t_kernel(
             nc.vector.scalar_tensor_tensor(
                 out=u[:].rearrange("h (r p) -> h r p", p=P),
                 in0=st[("s2", q, 2)][:].rearrange("h (r p) -> h r p", p=P),
-                scalar=bh[:, 2:3],
+                scalar=bhraw[2][:],
                 in1=ts_bc[c // 4][:, t0 + lo : t0 + hi].rearrange("h " + TOKENS[c] + " -> h r p", p=P),
                 op0=ALU.add,
                 op1=ALU.mult,
@@ -308,7 +304,7 @@ def tile_cfccell_pa_t_kernel(
         def Eb(q):
             v = work.tile([P, q[2] - q[1]], F32, name="v", tag="v", bufs=2)
             nc.vector.scalar_tensor_tensor(
-                out=v[:], in0=st[("u", q)][:], scalar=bh[:, 3:4], in1=st[("s2", q, 3)][:],
+                out=v[:], in0=st[("u", q)][:], scalar=bhraw[3][:], in1=st[("s2", q, 3)][:],
                 op0=ALU.add, op1=ALU.add,
             )
             st[("v", q)] = v
@@ -357,16 +353,18 @@ def tile_cfccell_pa_t_kernel(
             return 0 <= c < NB
 
         keep_busy(5)
-        for n in range(4):
-            w1_group(n, True)
-            if n > 0:
-                w1_quant(n - 1)
+        w1_group(0, True)
+        w1_group(1, True)
+        w1_quant(0, 1)
+        w1_group(2, True)
+        w1_group(3, False)
+        w1_quant(1, 2)
         T_in(0)
         keep_busy(4)
         new_grp(0)
         X_in(0, 0, False)
         X_in(0, 1, True)
-        w1_quant(3)
+        w1_quant(2, 4)
         b1_prep()
         Q1(0)
         for n in range(3):
@@ -376,8 +374,7 @@ def tile_cfccell_pa_t_kernel(
         w1_group(5, False)
         w1_group(6, True)
         w1_group(7, True)
-        for n in range(4, 8):
-            w1_quant(n)
+        w1_quant(4, 8)
 
         for i in range(NB - 1):
             q, b, a = WHOLE[i], i - 1, i - 2
@@ -410,8 +407,6 @@ def tile_cfccell_pa_t_kernel(
             P1(q, 6)
             if ok(a):
                 Em(WHOLE[a])
-            if i == 1:
-                bias_prep()
             if i < 2:
                 wh_group(2 - 2 * i)
                 wh_group(3 - 2 * i)

from contextlib import ExitStack

import concourse.bass as bass
import concourse.mybir as mybir
import concourse.tile as tile
from concourse.masks import make_identity

F32 = mybir.dt.float32
BF16 = mybir.dt.bfloat16
U32 = mybir.dt.uint32
U8 = mybir.dt.uint8
FP8X4 = mybir.dt.float8_e4m3fn_x4
AF = mybir.ActivationFunctionType
ALU = mybir.AluOpType

P = 128
NB, T, U, V, H = 8, 512, 512, 1024, 128
R = T // P
WHOLE = [(c, 0, T) for c in range(NB - 1)]
HALVES = [(NB - 1, 0, T // 2), (NB - 1, T // 2, T)]
V0 = 3
TOKENS = ["(p r)"] * V0 + ["(r p)"] * (NB - V0)
LECUN_A = 1.7159
LECUN_B = 0.666
FLOPS = 2 * NB * T * U * V + 2 * NB * T * V * 4 * H


def tile_cfccell_pa_t_kernel(
    tc, h1, ts, W1, b1, W_ff1, b_ff1, W_ff2, b_ff2, W_ta, b_ta, W_tb, b_tb, out
):
    nc = tc.nc
    with ExitStack() as ctx:
        const = ctx.enter_context(tc.tile_pool(name="const", bufs=1))
        work = ctx.enter_context(tc.tile_pool(name="work", bufs=3))
        psum = ctx.enter_context(tc.psum_pool(name="psum", bufs=1))
        ctx.enter_context(tc.manual_schedule())

        h1raw = [const.tile([P, R, U], BF16, name="h1raw%d" % c) for c in range(V0)]
        h1raw += [const.tile([P, 2, U], BF16, name="h1raw%d" % c) for c in range(V0, NB)]
        h1vec = {
            c: const.tile([P, 2 * U], BF16, name="h1vec%d" % c, align_bytes=64)
            for c in range(V0, NB)
        }
        w1raw = [const.tile([P, 4, V // 2], BF16, name="w1raw%d" % g) for g in range(2)]
        whraw = [const.tile([P, 2, 4, H], BF16, name="whraw%d" % k) for k in range(4)]
        ts_bc = [const.tile([P, 4 * T], BF16, name="ts_bc%d" % q) for q in range(2)]
        b1raw = const.tile([P, 8], BF16, name="b1raw")
        bhraw = [const.tile([P, 1], BF16, name="bhraw%d" % k) for k in range(4)]
        ts_flat = ts.rearrange("b t -> (b t)")
        heads = (W_ff1, W_ff2, W_ta, W_tb)

        def load_h1(c, r0, r1):
            nc.sync.dma_start(
                out=h1raw[c][:, r0:r1, :],
                in_=h1[c].rearrange(TOKENS[c] + " k -> p r k", p=P)[:, r0:r1, :],
            )

        def load_h1_both(c):
            if c < V0:
                load_h1(c, 0, 4)
                return
            load_h1(c, 0, 2)
            pieces = h1[c][T // 2 : T, :].rearrange("(b t) (u a j) -> a (t u) b j", b=16, u=2, a=4)
            for a in range(4):
                nc.sync.dma_start(
                    out=h1vec[c][32 * a : 32 * a + 32, :].rearrange("q (b j) -> q b j", b=16),
                    in_=pieces[a],
                )

        def load_w1(g):
            for u in range(2):
                nc.sync.dma_start(
                    out=w1raw[g][:, 2 * u : 2 * u + 2, :],
                    in_=W1[256 * u : 256 * u + 256, 512 * g : 512 * g + 512].rearrange(
                        "(p e) v -> p e v", e=2
                    ),
                )

        def load_wh(k):
            nc.sync.dma_start(
                out=whraw[k][:], in_=heads[k].rearrange("(g q j) n -> q g j n", g=2, j=4)
            )

        def load_ts(q):
            nc.sync.dma_start(
                out=ts_bc[q][:],
                in_=ts_flat[4 * T * q : 4 * T * q + 4 * T].partition_broadcast(P),
            )

        load_w1(0)
        load_h1(0, 0, 2)
        load_h1(0, 2, 4)
        with nc.allow_non_contiguous_dma(reason="b1, two runs of four elements to a partition"):
            nc.sync.dma_start(
                out=b1raw[:].rearrange("q (g j) -> q g j", g=2),
                in_=b1.rearrange("(g q j) -> q g j", g=2, j=4),
            )
        load_w1(1)
        load_h1_both(1)
        load_wh(2)
        load_wh(3)
        load_h1_both(2)
        load_wh(0)
        load_wh(1)
        load_ts(0)
        load_h1_both(3)

        ident = const.tile([P, P], F32, name="ident")
        make_identity(nc, ident[:])
        with nc.allow_non_contiguous_dma(reason="head biases, one element to a partition"):
            for k, b in enumerate((b_ff1, b_ff2, b_ta, b_tb)):
                nc.gpsimd.dma_start(out=bhraw[k][:], in_=b.rearrange("(q o) -> q o", o=1))
        warm = const.tile([P, 1], F32, name="warm")
        nc.vector.memset(warm[:], 0.0)
        warm2 = const.tile([P, 1], F32, name="warm2")
        nc.scalar.activation(out=warm2[:], in_=warm[:], func=AF.Tanh)

        zeros = const.tile([P, T], BF16, name="zeros")
        nc.vector.memset(zeros[:], 0.0)

        def keep_busy(count):
            for n in range(count):
                idle = psum.tile([P, T], F32, name="idle", tag="s1", bufs=3)
                nc.tensor.matmul(
                    out=idle[:], lhsT=zeros[:, 0:P], rhs=zeros[:], start=True, stop=True
                )

        w1grp = const.tile([P, V, 4], BF16, name="w1grp", align_bytes=256)
        w1c = const.tile([P, V], U32, name="w1c", align_bytes=256)
        w1s = const.tile([P, V], U8, name="w1s", align_bytes=256)
        whgrp = const.tile([P, 8, H, 4], BF16, name="whgrp", align_bytes=256)
        whc = const.tile([P, 8 * H], U32, name="whc", align_bytes=256)
        whs = const.tile([P, 8 * H], U8, name="whs", align_bytes=256)
        b1s = const.tile([P, 8], F32, name="b1s")
        nb_ff1 = const.tile([P, 1], F32, name="nb_ff1")

        def w1_group(n, on_vector):
            dst = w1grp[:, P * n : P * n + P, :].rearrange("p (c i) t -> p c t i", i=4)
            src = w1raw[n // 4][:].rearrange("p t (c i j) -> p j c t i", i=4, j=4)[:, n % 4]
            if on_vector:
                nc.vector.tensor_copy(out=dst, in_=src)
            else:
                nc.scalar.copy(out=dst, in_=src)

        def w1_quant(n0, n1):
            cols = slice(P * n0, P * n1)
            nc.vector.quantize_mx(
                out=w1c[:, cols].bitcast(FP8X4),
                scales=w1s[:, cols],
                in_=w1grp[:, cols, :].rearrange("p v t -> p (v t)"),
            )

        def wh_group(k):
            nc.vector.tensor_copy(
                out=whgrp[:, 2 * k : 2 * k + 2, :, :],
                in_=whraw[k][:].rearrange("p g j n -> p g n j"),
            )

        def wh_quant(pair):
            cols = slice(512 * pair, 512 * pair + 512)
            nc.vector.quantize_mx(
                out=whc[:, cols].bitcast(FP8X4),
                scales=whs[:, cols],
                in_=whgrp[:, 4 * pair : 4 * pair + 4, :, :].rearrange("p a n j -> p (a n j)"),
            )

        def b1_prep():
            nc.scalar.mul(out=b1s[:], in_=b1raw[:], mul=LECUN_B)

        nc.gpsimd.tensor_scalar(
            out=nb_ff1[:], in0=bhraw[0][:], scalar1=-1.0, scalar2=0.0, op0=ALU.mult, op1=ALU.add
        )

        st = {}

        def T_in(c):
            words = h1raw[c][:].bitcast(F32)
            for half in range(2 if c < V0 else 1):
                tr = psum.tile([P, 2, 256], F32, name="tr", tag="tr", bufs=3)
                for rr in range(2):
                    for u in range(2):
                        nc.tensor.transpose(
                            tr[:, u, P * rr : P * rr + P],
                            words[:, 2 * half + rr, P * u : P * u + P],
                            ident[:],
                        )
                st[("tr", c, half)] = tr

        def new_grp(c):
            st[("h1grp", c)] = work.tile(
                [P, T, 4], BF16, name="h1grp", tag="h1grp", bufs=2, align_bytes=256
            )

        def X_in(c, half, on_vector):
            dst = st[("h1grp", c)][:].bitcast(F32)[:, 256 * half : 256 * half + 256, :]
            src = st[("tr", c, half)][:].rearrange("p u w -> p w u")
            if on_vector:
                nc.vector.tensor_copy(out=dst, in_=src)
            else:
                nc.scalar.copy(out=dst, in_=src)

        def V_in(c):
            dst = st[("h1grp", c)][:].bitcast(F32)[:, 256:512, :].rearrange("p w u -> p (w u)")
            nc.vector.transpose(dst, h1vec[c][:].bitcast(F32))

        def Q1(c):
            h1c = work.tile([P, T], U32, name="h1c", tag="h1c", bufs=2, align_bytes=256)
            h1s = work.tile([P, T], U8, name="h1s", tag="h1s", bufs=2, align_bytes=256)
            nc.vector.quantize_mx(
                out=h1c[:].bitcast(FP8X4),
                scales=h1s[:],
                in_=st[("h1grp", c)][:].rearrange("p w t -> p (w t)"),
            )
            st[("h1c", c)] = (h1c, h1s)

        def P1(q, n):
            c, lo, hi = q
            h1c, h1s = st[("h1c", c)]
            acc = psum.tile([P, hi - lo], F32, name="s1", tag="s1", bufs=3)
            cols = slice(P * n, P * n + P)
            nc.tensor.matmul_mx(
                out=acc[:],
                lhsT=w1c[:, cols].bitcast(FP8X4),
                lhsT_scale=w1s[:, cols],
                rhs=h1c[:, lo:hi].bitcast(FP8X4),
                rhs_scale=h1s[:, lo:hi],
                start=True,
                stop=True,
            )
            st[("s1", q, n)] = acc

        def A1(q, n):
            g, j = n // 4, n % 4
            if j == 0:
                st[("th1", q, g)] = work.tile([P, 4, q[2] - q[1]], F32, name="th1", tag="th1", bufs=4)
            nc.scalar.activation(
                out=st[("th1", q, g)][:, j, :],
                in_=st[("s1", q, n)][:],
                func=AF.Tanh,
                bias=b1s[:, n : n + 1],
                scale=LECUN_B,
            )

        def M(q, g):
            xgrp = work.tile([P, q[2] - q[1], 4], BF16, name="xgrp", tag="xgrp", bufs=3, align_bytes=256)
            nc.vector.tensor_scalar(
                out=xgrp[:].rearrange("p (c i) j -> p c j i", i=4),
                in0=st[("th1", q, g)][:].rearrange("p j (c i) -> p c j i", i=4),
                scalar1=LECUN_A,
                scalar2=None,
                op0=ALU.mult,
            )
            st[("xgrp", q, g)] = xgrp

        def Q2(q, g):
            xc = work.tile([P, q[2] - q[1]], U32, name="xc", tag="xc%d" % g, bufs=3, align_bytes=256)
            xs = work.tile([P, q[2] - q[1]], U8, name="xs", tag="xs%d" % g, bufs=3, align_bytes=256)
            nc.vector.quantize_mx(
                out=xc[:].bitcast(FP8X4),
                scales=xs[:],
                in_=st[("xgrp", q, g)][:].rearrange("p w t -> p (w t)"),
            )
            st[("xc", q, g)] = (xc, xs)

        def S2(q, k, tag="s2", bufs=2):
            acc = psum.tile([P, q[2] - q[1]], F32, name="s2", tag=tag, bufs=bufs)
            for g in range(2):
                xc, xs = st[("xc", q, g)]
                cols = slice(P * (2 * k + g), P * (2 * k + g) + P)
                nc.tensor.matmul_mx(
                    out=acc[:],
                    lhsT=whc[:, cols].bitcast(FP8X4),
                    lhsT_scale=whs[:, cols],
                    rhs=xc[:].bitcast(FP8X4),
                    rhs_scale=xs[:],
                    start=(g == 0),
                    stop=(g == 1),
                )
            st[("s2", q, k)] = acc

        def FF(q, k):
            ff = work.tile([P, q[2] - q[1]], F32, name="ff", tag="ff%d" % k, bufs=2)
            nc.scalar.activation(
                out=ff[:], in_=st[("s2", q, k)][:], func=AF.Tanh,
                bias=(nb_ff1 if k == 0 else bhraw[1])[:],
                scale=(-1.0 if k == 0 else 1.0),
            )
            st[("ff", q, k)] = ff

        def Ea(q):
            u = work.tile([P, q[2] - q[1]], F32, name="u", tag="u", bufs=2)
            c, lo, hi = q
            t0 = T * (c % 4)
            nc.vector.scalar_tensor_tensor(
                out=u[:].rearrange("h (r p) -> h r p", p=P),
                in0=st[("s2", q, 2)][:].rearrange("h (r p) -> h r p", p=P),
                scalar=bhraw[2][:],
                in1=ts_bc[c // 4][:, t0 + lo : t0 + hi].rearrange("h " + TOKENS[c] + " -> h r p", p=P),
                op0=ALU.add,
                op1=ALU.mult,
            )
            st[("u", q)] = u

        def Eb(q):
            v = work.tile([P, q[2] - q[1]], F32, name="v", tag="v", bufs=2)
            nc.vector.scalar_tensor_tensor(
                out=v[:], in0=st[("u", q)][:], scalar=bhraw[3][:], in1=st[("s2", q, 3)][:],
                op0=ALU.add, op1=ALU.add,
            )
            st[("v", q)] = v

        def turn(dst, src, start, stop):
            nc.tensor.matmul(
                out=dst, lhsT=src, rhs=ident[:], start=start, stop=stop, is_transpose=True
            )

        def T_out(q):
            v_t = psum.tile([P, (q[2] - q[1]) // P, H], F32, name="v_t", tag="tr", bufs=3)
            d_t = psum.tile([P, (q[2] - q[1]) // P, H], F32, name="d_t", tag="tr", bufs=3)
            n_t = psum.tile([P, (q[2] - q[1]) // P, H], F32, name="n_t", tag="tr", bufs=3)
            for r in range((q[2] - q[1]) // P):
                turn(v_t[:, r, :], st[("v", q)][:, P * r : P * r + P], True, True)
            for r in range((q[2] - q[1]) // P):
                turn(d_t[:, r, :], st[("ff", q, 0)][:, P * r : P * r + P], True, False)
                turn(d_t[:, r, :], st[("ff", q, 1)][:, P * r : P * r + P], False, True)
            for r in range((q[2] - q[1]) // P):
                turn(n_t[:, r, :], st[("ff", q, 0)][:, P * r : P * r + P], True, True)
            st[("out", q)] = (v_t, d_t, n_t)

        def TH(q):
            th = work.tile([P, (q[2] - q[1]) // P, H], F32, name="th", tag="th", bufs=2)
            nc.scalar.activation(out=th[:], in_=st[("out", q)][0][:], func=AF.Tanh, scale=0.5)
            st[("th", q)] = th

        def Em(q):
            e = work.tile([P, (q[2] - q[1]) // P, H], F32, name="e", tag="e", bufs=2)
            nc.vector.scalar_tensor_tensor(
                out=e[:], in0=st[("th", q)][:], scalar=1.0, in1=st[("out", q)][1][:],
                op0=ALU.add, op1=ALU.mult,
            )
            st[("e", q)] = e

        def Eo(q):
            osb = work.tile([P, (q[2] - q[1]) // P, H], F32, name="osb", tag="osb", bufs=3)
            nc.vector.scalar_tensor_tensor(
                out=osb[:], in0=st[("e", q)][:], scalar=0.5, in1=st[("out", q)][2][:],
                op0=ALU.mult, op1=ALU.subtract,
            )
            c, lo, hi = q
            nc.sync.dma_start(out=out[c][lo:hi].rearrange(TOKENS[c] + " h -> p r h", p=P), in_=osb[:])

        def ok(c):
            return 0 <= c < NB

        keep_busy(5)
        w1_group(0, True)
        w1_group(1, True)
        w1_quant(0, 1)
        w1_group(2, True)
        w1_group(3, False)
        w1_quant(1, 2)
        T_in(0)
        keep_busy(4)
        new_grp(0)
        X_in(0, 0, False)
        X_in(0, 1, True)
        w1_quant(2, 4)
        b1_prep()
        Q1(0)
        for n in range(3):
            P1(WHOLE[0], n)
        T_in(1)
        w1_group(4, False)
        w1_group(5, False)
        w1_group(6, True)
        w1_group(7, True)
        w1_quant(4, 8)

        for i in range(NB - 1):
            q, b, a = WHOLE[i], i - 1, i - 2
            if ok(i + 4):
                load_h1_both(i + 4)
            if i == 0:
                load_ts(1)
            if ok(a):
                T_out(WHOLE[a])
            A1(q, 0)
            P1(q, 3)
            if ok(b):
                M(WHOLE[b], 0)
                M(WHOLE[b], 1)
                Q2(WHOLE[b], 0)
                Q2(WHOLE[b], 1)
            A1(q, 1)
            P1(q, 4)
            if ok(a):
                TH(WHOLE[a])
            if 1 <= i:
                T_in(i + 1)
            if ok(b):
                S2(WHOLE[b], 2)
            A1(q, 2)
            P1(q, 5)
            if ok(b):
                S2(WHOLE[b], 3)
            A1(q, 3)
            P1(q, 6)
            if ok(a):
                Em(WHOLE[a])
            if i < 2:
                wh_group(2 - 2 * i)
                wh_group(3 - 2 * i)
            if ok(i + 1):
                new_grp(i + 1)
                X_in(i + 1, 0, False)
                if i + 1 < V0:
                    X_in(i + 1, 1, i == 0)
                else:
                    V_in(i + 1)
            if ok(a):
                Eo(WHOLE[a])
            A1(q, 4)
            P1(q, 7)
            if ok(b):
                Ea(WHOLE[b])
            if i < 2:
                wh_quant(1 - i)
            if ok(i + 1):
                Q1(i + 1)
            if ok(b):
                Eb(WHOLE[b])
                S2(WHOLE[b], 0)
                S2(WHOLE[b], 1)
            for n in range(3):
                A1(q, 5 + n)
                if ok(i + 1):
                    P1((WHOLE + HALVES)[i + 1], n)
            if ok(b):
                FF(WHOLE[b], 0)
                FF(WHOLE[b], 1)

        z, a = WHOLE[-2:]
        x, y = HALVES
        T_out(z)
        A1(x, 0)
        P1(x, 3)
        M(a, 0)
        M(a, 1)
        Q2(a, 0)
        Q2(a, 1)
        A1(x, 1)
        P1(x, 4)
        A1(x, 2)
        P1(x, 5)
        TH(z)
        S2(a, 2)
        A1(x, 3)
        P1(x, 6)
        A1(x, 4)
        P1(x, 7)
        S2(a, 3)
        Em(z)
        A1(x, 5)
        P1(y, 0)
        M(x, 0)
        A1(x, 6)
        P1(y, 1)
        Eo(z)
        A1(x, 7)
        P1(y, 2)
        Ea(a)
        A1(y, 0)
        P1(y, 3)
        A1(y, 1)
        P1(y, 4)
        S2(a, 0)
        M(x, 1)
        Eb(a)
        A1(y, 2)
        P1(y, 5)
        A1(y, 3)
        P1(y, 6)
        Q2(x, 0)
        A1(y, 4)
        P1(y, 7)
        S2(a, 1)
        Q2(x, 1)
        A1(y, 5)
        A1(y, 6)
        A1(y, 7)
        S2(x, 2, "s1", 3)
        S2(x, 3, "s1", 3)
        M(y, 0)
        FF(a, 0)
        M(y, 1)
        FF(a, 1)
        Q2(y, 0)
        T_out(a)
        TH(a)
        Ea(x)
        Q2(y, 1)
        S2(x, 0)
        S2(x, 1)
        S2(y, 2, "s1", 3)
        S2(y, 3, "s1", 3)
        Eb(x)
        FF(x, 0)
        FF(x, 1)
        S2(y, 0)
        S2(y, 1)
        Em(a)
        Ea(y)
        Eo(a)
        T_out(x)
        TH(x)
        Eb(y)
        FF(y, 0)
        FF(y, 1)
        Em(x)
        Eo(x)
        T_out(y)
        TH(y)
        Em(y)
        Eo(y)
